import numpy as np
import ml_dtypes


def mxq(x, axis, fmt="e4m3"):
    dtype, down = {"e4m3": (ml_dtypes.float8_e4m3fn, 7), "e5m2": (ml_dtypes.float8_e5m2, 14)}[fmt]
    v = np.moveaxis(np.asarray(x, np.float32).astype(ml_dtypes.bfloat16).astype(np.float64), axis, -1)
    blocks = v.reshape(v.shape[:-1] + (-1, 32))
    amax = np.abs(blocks).max(-1, keepdims=True)
    byte = np.maximum(np.where(amax > 0, np.frexp(amax)[1] - 1 + 127, 0) - down, 1)
    scale = np.exp2(byte - 127.0)
    codes = (blocks / scale).astype(np.float32).astype(dtype).astype(np.float64)
    return np.moveaxis((codes * scale).reshape(v.shape), -1, axis)


WIDE = False


def mx_kscale(k):
    if not WIDE:
        return np.ones(k)
    levels = np.array([10, -10, 5, -5, 0])
    a = np.random.permutation(np.resize(levels, k // 512 * 4)).reshape(k // 512, 4)
    idx = np.arange(k)
    return np.exp2(a[idx // 512, idx % 128 // 32])


BF16 = ml_dtypes.bfloat16


def bf(x):
    return np.asarray(x, np.float32).astype(BF16)


def f64(x):
    return np.asarray(x).astype(np.float64)


B, L, H, D = 2, 512, 8, 128
DIM = H * D


def sigmoid(a):
    return 1.0 / (1.0 + np.exp(-a))


def setup_inputs():
    r = np.random.standard_normal
    s = mx_kscale(DIM)
    return {"q_rot_re": bf(r((B, L, H, D)) * 0.36),
            "q_rot_im": bf(r((B, L, H, D)) * 0.36),
            "k_rot_re": bf(r((B, L, H, D)) * 0.36),
            "k_rot_im": bf(r((B, L, H, D)) * 0.36),
            "x": bf(r((B, L, DIM)) * s),
            "wv_w": bf(r((DIM, DIM)) * 0.5 / np.sqrt(DIM) / s[None, :]),
            "wv_b": bf(r(DIM) * 0.1),
            "amplitude": bf(3.5 + 0.5 * r(H))}


def reference(q_rot_re, q_rot_im, k_rot_re, k_rot_im, x, wv_w, wv_b, amplitude):
    v = (mxq(f64(x), 2, "e4m3") @ mxq(f64(wv_w), 1, "e4m3").T) + f64(wv_b)
    v = v.reshape(B, L, H, D).transpose(0, 2, 1, 3)
    qk_re = (f64(q_rot_re).transpose(0, 2, 1, 3) @ f64(k_rot_re).transpose(0, 2, 3, 1)
             - f64(q_rot_im).transpose(0, 2, 1, 3) @ f64(k_rot_im).transpose(0, 2, 3, 1))
    amp = sigmoid(f64(amplitude))
    t = np.arange(L)
    diff = t[:, None] - t[None, :]
    tril = diff >= 0
    decay = np.where(tril[None], amp[:, None, None] ** np.where(tril, diff, 0)[None], 0.0)
    p = qk_re * decay[None]
    inner = mxq(p, 3, "e4m3") @ mxq(v, 2, "e4m3")
    return inner.transpose(0, 2, 1, 3).reshape(B, L, DIM)

@@ -1,0 +1,257 @@
+from contextlib import ExitStack
+
+import concourse.mybir as mybir
+from concourse.masks import make_identity
+
+BF16 = mybir.dt.bfloat16
+F32 = mybir.dt.float32
+I32 = mybir.dt.int32
+U32 = mybir.dt.uint32
+U8 = mybir.dt.uint8
+FP8X4 = mybir.dt.float8_e4m3fn_x4
+ACT = mybir.ActivationFunctionType
+ALU = mybir.AluOpType
+
+P = 128
+PACK = 4
+B, L, H, D = 2, 512, 8, 128
+DIM = H * D
+TILES = L // P
+ROW_TILES = B * TILES
+PASSES = DIM // (P * PACK)
+HEAD_GROUP = 4
+
+FLOPS = 2 * B * L * DIM * DIM + 2 * B * H * L * L * (2 * D) + 2 * B * H * L * L * D
+
+
+def tile_retention_pb_kernel(
+    tc, q_rot_re, q_rot_im, k_rot_re, k_rot_im, x, wv_w, wv_b, amplitude, out
+):
+    nc = tc.nc
+    with ExitStack() as ctx:
+        const = ctx.enter_context(tc.tile_pool(name="const", bufs=1))
+        inputs = ctx.enter_context(tc.tile_pool(name="inputs", bufs=1))
+        keep = ctx.enter_context(tc.tile_pool(name="keep", bufs=1))
+        stage = ctx.enter_context(tc.tile_pool(name="stage", bufs=3))
+        psum = ctx.enter_context(tc.psum_pool(name="psum", bufs=1))
+
+        def load_rows(name, rows):
+            resident = inputs.tile([P, ROW_TILES, DIM], BF16, name=name)
+            return resident, rows.rearrange("(n p) c -> p n c", p=P)
+
+        x_sb, x_rows = load_rows("x_sb", x.rearrange("b l k -> (b l) k"))
+        w_sb, w_rows = load_rows("w_sb", wv_w)
+        rotated = {}
+        for name, tensor in (
+            ("q_re", q_rot_re),
+            ("q_im", q_rot_im),
+            ("k_re", k_rot_re),
+            ("k_im", k_rot_im),
+        ):
+            rotated[name] = load_rows(name, tensor.rearrange("b l h d -> (b l) (h d)"))
+
+        for n in range(TILES):
+            nc.sync.dma_start(out=x_sb[:, n, :], in_=x_rows[:, n, :])
+        for n in range(ROW_TILES):
+            nc.sync.dma_start(out=w_sb[:, n, :], in_=w_rows[:, n, :])
+        for n in range(TILES, ROW_TILES):
+            nc.sync.dma_start(out=x_sb[:, n, :], in_=x_rows[:, n, :])
+        for n in range(ROW_TILES):
+            for name in ("q_re", "q_im", "k_re", "k_im"):
+                resident, rows = rotated[name]
+                nc.sync.dma_start(out=resident[:, n, :], in_=rows[:, n, :])
+
+        ident_f32 = const.tile([P, P], F32)
+        make_identity(nc, ident_f32[:])
+        ident_bf16 = const.tile([P, P], BF16)
+        make_identity(nc, ident_bf16[:])
+
+        bias_all = const.tile([P, DIM], BF16)
+        nc.scalar.dma_start(out=bias_all[:], in_=wv_b.partition_broadcast(P))
+        amplitude_all = const.tile([P, H], BF16)
+        nc.scalar.dma_start(out=amplitude_all[:], in_=amplitude.partition_broadcast(P))
+
+        log_amp = const.tile([P, H], F32)
+        nc.scalar.activation(out=log_amp[:], in_=amplitude_all[:], func=ACT.Sigmoid)
+        nc.scalar.activation(out=log_amp[:], in_=log_amp[:], func=ACT.Ln)
+
+        farthest = (TILES - 1) * P
+        distance_pattern = [[1, P], [-P, TILES]]
+        distance_int = const.tile([P, P * TILES], I32)
+        nc.gpsimd.iota(
+            distance_int[:], pattern=distance_pattern, base=farthest, channel_multiplier=-1
+        )
+        distance = const.tile([P, P * TILES], F32)
+        nc.vector.tensor_copy(out=distance[:], in_=distance_int[:])
+        nc.vector.tensor_scalar_max(out=distance[:], in0=distance[:], scalar1=0.0)
+        decay = const.tile([P, H, P, TILES], F32)
+        for h in range(H):
+            decay_h = decay[:, h].rearrange("p c u -> p (c u)")
+            nc.scalar.activation(
+                out=decay_h, in_=distance[:], func=ACT.Exp, scale=log_amp[:, h : h + 1]
+            )
+            nc.gpsimd.affine_select(
+                out=decay_h,
+                in_=decay_h,
+                pattern=distance_pattern,
+                compare_op=ALU.is_ge,
+                fill=0.0,
+                base=farthest,
+                channel_multiplier=-1,
+            )
+
+        p_grouped_ring = []
+        for slot in range(3):
+            p_grouped = keep.tile([P, L, PACK], BF16, name="p_grouped%d" % slot, align_bytes=64)
+            nc.vector.memset(p_grouped[:].bitcast(I32), 0)
+            p_grouped_ring.append(p_grouped)
+
+        x_codes = keep.tile([P, ROW_TILES, PASSES, P], U32, align_bytes=64)
+        x_scales = keep.tile([P, ROW_TILES, PASSES, P], U8, align_bytes=64)
+        w_codes = keep.tile([P, ROW_TILES, PASSES, P], U32, align_bytes=64)
+        w_scales = keep.tile([P, ROW_TILES, PASSES, P], U8, align_bytes=64)
+        v_codes = keep.tile([P, B, H, D], U32, align_bytes=64)
+        v_scales = keep.tile([P, B, H, D], U8, align_bytes=64)
+
+        def quantise_rows(rows_sb, codes, scales):
+            words = rows_sb.bitcast(F32)
+            flipped = psum.tile([P, PASSES, 2, P], F32, tag="flip", bufs=2)
+            for g in range(PASSES):
+                for u in range(2):
+                    first = (2 * g + u) * P
+                    nc.tensor.transpose(
+                        flipped[:, g, u, :], words[:, first : first + P], ident_f32[:]
+                    )
+            grouped = stage.tile([P, PASSES, P, PACK], BF16, align_bytes=64)
+            nc.scalar.copy(
+                out=grouped[:].bitcast(F32), in_=flipped[:].rearrange("p g u r -> p g r u")
+            )
+            nc.vector.quantize_mx(
+                out=codes.rearrange("p g r -> p (g r)").bitcast(FP8X4),
+                scales=scales.rearrange("p g r -> p (g r)"),
+                in_=grouped[:].rearrange("p g r t -> p (g r t)"),
+            )
+
+        def project_values(b, h):
+            v_acc = psum.tile([P, TILES, D], F32, tag="quad", bufs=6)
+            for j in range(TILES):
+                for g in range(PASSES):
+                    nc.tensor.matmul_mx(
+                        out=v_acc[:, j, :],
+                        lhsT=x_codes[:, b * TILES + j, g, :].bitcast(FP8X4),
+                        lhsT_scale=x_scales[:, b * TILES + j, g, :],
+                        rhs=w_codes[:, h, g, :].bitcast(FP8X4),
+                        rhs_scale=w_scales[:, h, g, :],
+                        start=(g == 0),
+                        stop=(g == PASSES - 1),
+                    )
+            v_grouped = stage.tile([P, D, PACK], BF16, align_bytes=64)
+            nc.vector.tensor_tensor(
+                out=v_grouped[:],
+                in0=v_acc[:].rearrange("p j d -> p d j"),
+                in1=bias_all[:, h * D : (h + 1) * D].unsqueeze(2).to_broadcast([P, D, PACK]),
+                op=ALU.add,
+            )
+            nc.vector.quantize_mx(
+                out=v_codes[:, b, h, :].bitcast(FP8X4),
+                scales=v_scales[:, b, h, :],
+                in_=v_grouped[:].rearrange("p d j -> p (d j)"),
+            )
+
+        for n in range(TILES):
+            quantise_rows(x_sb[:, n, :], x_codes[:, n], x_scales[:, n])
+        for n in range(ROW_TILES):
+            quantise_rows(w_sb[:, n, :], w_codes[:, n], w_scales[:, n])
+        for n in range(TILES, ROW_TILES):
+            quantise_rows(x_sb[:, n, :], x_codes[:, n], x_scales[:, n])
+        for b in range(B):
+            for h in range(H):
+                project_values(b, h)
+
+        def flip_head(b, h):
+            channels_first = {}
+            for side in ("q", "k"):
+                flipped = psum.tile([P, 2, L], BF16, tag="flip", bufs=2)
+                for part, name in enumerate((side + "_re", side + "_im")):
+                    resident = rotated[name][0]
+                    for t in range(TILES):
+                        nc.tensor.transpose(
+                            flipped[:, part, t * P : (t + 1) * P],
+                            resident[:, b * TILES + t, h * D : (h + 1) * D],
+                            ident_bf16[:],
+                        )
+                channels_first[side] = stage.tile([P, 2, L], BF16, name=side + "T")
+                if side == "q":
+                    nc.scalar.copy(out=channels_first[side][:], in_=flipped[:])
+                else:
+                    nc.scalar.copy(out=channels_first[side][:, 0, :], in_=flipped[:, 0, :])
+                    nc.scalar.mul(out=channels_first[side][:, 1, :], in_=flipped[:, 1, :], mul=-1.0)
+            return channels_first
+
+        def score_head(h, channels_first, p_grouped):
+            qT, kT = channels_first["q"], channels_first["k"]
+            for i in range(TILES):
+                s_acc = psum.tile([P, TILES, P], F32, tag="quad", bufs=6)
+                for j in range(i + 1):
+                    for part in range(2):
+                        nc.tensor.matmul(
+                            out=s_acc[:, j, :],
+                            lhsT=kT[:, part, j * P : (j + 1) * P],
+                            rhs=qT[:, part, i * P : (i + 1) * P],
+                            start=(part == 0),
+                            stop=(part == 1),
+                        )
+                nc.vector.tensor_tensor(
+                    out=p_grouped[:, i * P : (i + 1) * P, 0 : i + 1],
+                    in0=s_acc[:, 0 : i + 1, :].rearrange("p j c -> p c j"),
+                    in1=decay[:, h, :, TILES - 1 - i : TILES],
+                    op=ALU.mult,
+                )
+            p_codes = stage.tile([P, L], U32, align_bytes=64)
+            p_scales = stage.tile([P, L], U8, align_bytes=64)
+            nc.vector.quantize_mx(
+                out=p_codes[:].bitcast(FP8X4),
+                scales=p_scales[:],
+                in_=p_grouped[:].rearrange("p l j -> p (l j)"),
+            )
+            return p_codes, p_scales
+
+        out_rows = out.rearrange("b (i p) c -> b p i c", p=P)
+        results = {}
+
+        def attend_head(b, h, p_codes, p_scales):
+            o_acc = psum.tile([P, TILES, D], F32, tag="quad", bufs=6)
+            for i in range(TILES):
+                nc.tensor.matmul_mx(
+                    out=o_acc[:, i, :],
+                    lhsT=p_codes[:, i * P : (i + 1) * P].bitcast(FP8X4),
+                    lhsT_scale=p_scales[:, i * P : (i + 1) * P],
+                    rhs=v_codes[:, b, h, :].bitcast(FP8X4),
+                    rhs_scale=v_scales[:, b, h, :],
+                    start=True,
+                    stop=True,
+                )
+            member = h % HEAD_GROUP
+            if member == 0:
+                results["tile"] = stage.tile([P, TILES, HEAD_GROUP, D], F32, name="result", bufs=2)
+            result = results["tile"]
+            nc.scalar.copy(out=result[:, :, member, :], in_=o_acc[:])
+            if member == HEAD_GROUP - 1:
+                first = (h - member) * D
+                nc.sync.dma_start(
+                    out=out_rows[b][:, :, first : first + HEAD_GROUP * D],
+                    in_=result[:].rearrange("p i g d -> p i (g d)"),
+                )
+
+        heads = [(b, h) for b in range(B) for h in range(H)]
+        flipped_of = {}
+        quantised_of = {}
+        for n in range(len(heads) + 2):
+            if n < len(heads):
+                flipped_of[n] = flip_head(*heads[n])
+            if 1 <= n <= len(heads):
+                quantised_of[n - 1] = score_head(
+                    heads[n - 1][1], flipped_of[n - 1], p_grouped_ring[(n - 1) % 3]
+                )
+            if n >= 2:
+                attend_head(*heads[n - 2], *quantised_of[n - 2])

@@ -19,7 +19,9 @@ DIM = H * D
 TILES = L // P
 ROW_TILES = B * TILES
 PASSES = DIM // (P * PACK)
-HEAD_GROUP = 4
+BANK = 512
+PAIR = 2
+EARLY = 2
 
 FLOPS = 2 * B * L * DIM * DIM + 2 * B * H * L * L * (2 * D) + 2 * B * H * L * L * D
 
@@ -28,19 +30,37 @@ def tile_retention_pb_kernel(
     tc, q_rot_re, q_rot_im, k_rot_re, k_rot_im, x, wv_w, wv_b, amplitude, out
 ):
     nc = tc.nc
+    heads = [(b, h) for b in range(B) for h in range(H)]
     with ExitStack() as ctx:
+        ctx.enter_context(tc.manual_schedule())
         const = ctx.enter_context(tc.tile_pool(name="const", bufs=1))
         inputs = ctx.enter_context(tc.tile_pool(name="inputs", bufs=1))
         keep = ctx.enter_context(tc.tile_pool(name="keep", bufs=1))
-        stage = ctx.enter_context(tc.tile_pool(name="stage", bufs=3))
+        stage = ctx.enter_context(tc.tile_pool(name="stage", bufs=2))
         psum = ctx.enter_context(tc.psum_pool(name="psum", bufs=1))
 
-        def load_rows(name, rows):
-            resident = inputs.tile([P, ROW_TILES, DIM], BF16, name=name)
-            return resident, rows.rearrange("(n p) c -> p n c", p=P)
+        amplitude_all = const.tile([P, H], BF16)
+        nc.scalar.dma_start(out=amplitude_all[:], in_=amplitude.partition_broadcast(P))
+        bias_row = const.tile([P, DIM], BF16)
+        nc.vector.memset(bias_row[:].bitcast(I32), 0)
+        nc.scalar.dma_start(out=bias_row[0:1, :], in_=wv_b.rearrange("(o c) -> o c", o=1))
+        ones = const.tile([P, P], BF16)
+        nc.vector.memset(ones[:], 1.0)
 
-        x_sb, x_rows = load_rows("x_sb", x.rearrange("b l k -> (b l) k"))
-        w_sb, w_rows = load_rows("w_sb", wv_w)
+        p_grouped_ring = []
+        for slot in range(3):
+            p_grouped = keep.tile([P, L, PACK], BF16, name="p_grouped%d" % slot, align_bytes=64)
+            nc.vector.memset(p_grouped[:].bitcast(I32), 0)
+            p_grouped_ring.append(p_grouped)
+
+        def resident_rows(name, rows):
+            return (
+                inputs.tile([P, ROW_TILES, DIM], BF16, name=name),
+                rows.rearrange("(n p) c -> p n c", p=P),
+            )
+
+        x_sb, x_rows = resident_rows("x_sb", x.rearrange("b l k -> (b l) k"))
+        w_sb, w_rows = resident_rows("w_sb", wv_w)
         rotated = {}
         for name, tensor in (
             ("q_re", q_rot_re),
@@ -48,32 +68,23 @@ def tile_retention_pb_kernel(
             ("k_re", k_rot_re),
             ("k_im", k_rot_im),
         ):
-            rotated[name] = load_rows(name, tensor.rearrange("b l h d -> (b l) (h d)"))
+            rotated[name] = resident_rows(name, tensor.rearrange("b l h d -> (b l) (h d)"))
 
-        for n in range(TILES):
-            nc.sync.dma_start(out=x_sb[:, n, :], in_=x_rows[:, n, :])
-        for n in range(ROW_TILES):
-            nc.sync.dma_start(out=w_sb[:, n, :], in_=w_rows[:, n, :])
-        for n in range(TILES, ROW_TILES):
-            nc.sync.dma_start(out=x_sb[:, n, :], in_=x_rows[:, n, :])
-        for n in range(ROW_TILES):
-            for name in ("q_re", "q_im", "k_re", "k_im"):
-                resident, rows = rotated[name]
-                nc.sync.dma_start(out=resident[:, n, :], in_=rows[:, n, :])
+        for b in range(B):
+            for n in range(b * TILES, (b + 1) * TILES):
+                nc.sync.dma_start(out=x_sb[:, n, :], in_=x_rows[:, n, :])
+            for first_head in range(0, H, PAIR):
+                if b == 0:
+                    for n in range(first_head, first_head + PAIR):
+                        nc.sync.dma_start(out=w_sb[:, n, :], in_=w_rows[:, n, :])
+                slots = slice(b * TILES, (b + 1) * TILES)
+                cols = slice(first_head * D, (first_head + PAIR) * D)
+                for name in ("q_re", "q_im", "k_re", "k_im"):
+                    resident, rows = rotated[name]
+                    nc.sync.dma_start(out=resident[:, slots, cols], in_=rows[:, slots, cols])
 
         ident_f32 = const.tile([P, P], F32)
         make_identity(nc, ident_f32[:])
-        ident_bf16 = const.tile([P, P], BF16)
-        make_identity(nc, ident_bf16[:])
-
-        bias_all = const.tile([P, DIM], BF16)
-        nc.scalar.dma_start(out=bias_all[:], in_=wv_b.partition_broadcast(P))
-        amplitude_all = const.tile([P, H], BF16)
-        nc.scalar.dma_start(out=amplitude_all[:], in_=amplitude.partition_broadcast(P))
-
-        log_amp = const.tile([P, H], F32)
-        nc.scalar.activation(out=log_amp[:], in_=amplitude_all[:], func=ACT.Sigmoid)
-        nc.scalar.activation(out=log_amp[:], in_=log_amp[:], func=ACT.Ln)
 
         farthest = (TILES - 1) * P
         distance_pattern = [[1, P], [-P, TILES]]
@@ -81,11 +92,18 @@ def tile_retention_pb_kernel(
         nc.gpsimd.iota(
             distance_int[:], pattern=distance_pattern, base=farthest, channel_multiplier=-1
         )
+        ident_bf16 = const.tile([P, P], BF16)
+        make_identity(nc, ident_bf16[:])
         distance = const.tile([P, P * TILES], F32)
         nc.vector.tensor_copy(out=distance[:], in_=distance_int[:])
         nc.vector.tensor_scalar_max(out=distance[:], in0=distance[:], scalar1=0.0)
+
+        log_amp = const.tile([P, H], F32)
+        nc.scalar.activation(out=log_amp[:], in_=amplitude_all[:], func=ACT.Sigmoid)
+        nc.scalar.activation(out=log_amp[:], in_=log_amp[:], func=ACT.Ln)
         decay = const.tile([P, H, P, TILES], F32)
-        for h in range(H):
+
+        def build_decay(h):
             decay_h = decay[:, h].rearrange("p c u -> p (c u)")
             nc.scalar.activation(
                 out=decay_h, in_=distance[:], func=ACT.Exp, scale=log_amp[:, h : h + 1]
@@ -100,11 +118,12 @@ def tile_retention_pb_kernel(
                 channel_multiplier=-1,
             )
 
-        p_grouped_ring = []
-        for slot in range(3):
-            p_grouped = keep.tile([P, L, PACK], BF16, name="p_grouped%d" % slot, align_bytes=64)
-            nc.vector.memset(p_grouped[:].bitcast(I32), 0)
-            p_grouped_ring.append(p_grouped)
+        bias_all = const.tile([P, DIM], BF16)
+        for half in range(DIM // BANK):
+            cols = slice(half * BANK, (half + 1) * BANK)
+            spread = psum.tile([P, BANK], F32, tag="late%d" % half)
+            nc.tensor.matmul(out=spread[:], lhsT=ones[:], rhs=bias_row[:, cols], start=True, stop=True)
+            nc.vector.tensor_copy(out=bias_all[:, cols], in_=spread[:])
 
         x_codes = keep.tile([P, ROW_TILES, PASSES, P], U32, align_bytes=64)
         x_scales = keep.tile([P, ROW_TILES, PASSES, P], U8, align_bytes=64)
@@ -113,27 +132,84 @@ def tile_retention_pb_kernel(
         v_codes = keep.tile([P, B, H, D], U32, align_bytes=64)
         v_scales = keep.tile([P, B, H, D], U8, align_bytes=64)
 
-        def quantise_rows(rows_sb, codes, scales):
+        def flip_rows(rows_sb, copy):
             words = rows_sb.bitcast(F32)
-            flipped = psum.tile([P, PASSES, 2, P], F32, tag="flip", bufs=2)
+            flipped = psum.tile([P, PASSES, 2, P], F32, tag="flip", bufs=3)
             for g in range(PASSES):
                 for u in range(2):
                     first = (2 * g + u) * P
                     nc.tensor.transpose(
                         flipped[:, g, u, :], words[:, first : first + P], ident_f32[:]
                     )
-            grouped = stage.tile([P, PASSES, P, PACK], BF16, align_bytes=64)
-            nc.scalar.copy(
-                out=grouped[:].bitcast(F32), in_=flipped[:].rearrange("p g u r -> p g r u")
-            )
+            grouped = stage.tile([P, PASSES, P, PACK], BF16, align_bytes=64, bufs=4)
+            copy(out=grouped[:].bitcast(F32), in_=flipped[:].rearrange("p g u r -> p g r u"))
+            return grouped
+
+        def quantise_rows(grouped, codes, scales):
             nc.vector.quantize_mx(
                 out=codes.rearrange("p g r -> p (g r)").bitcast(FP8X4),
                 scales=scales.rearrange("p g r -> p (g r)"),
                 in_=grouped[:].rearrange("p g r t -> p (g r t)"),
             )
 
+        def flip_head(b, h):
+            channels_first = {}
+            for side in ("q", "k"):
+                flipped = psum.tile([P, 2, L], BF16, tag="flip", bufs=3)
+                for part, name in enumerate((side + "_re", side + "_im")):
+                    resident = rotated[name][0]
+                    for t in range(TILES):
+                        nc.tensor.transpose(
+                            flipped[:, part, t * P : (t + 1) * P],
+                            resident[:, b * TILES + t, h * D : (h + 1) * D],
+                            ident_bf16[:],
+                        )
+                channels_first[side] = stage.tile([P, 2, L], BF16, name=side + "T", bufs=3)
+                if side == "q":
+                    nc.vector.tensor_copy(out=channels_first[side][:], in_=flipped[:])
+                else:
+                    nc.scalar.copy(out=channels_first[side][:, 0, :], in_=flipped[:, 0, :])
+                    nc.scalar.mul(out=channels_first[side][:, 1, :], in_=flipped[:, 1, :], mul=-1.0)
+            return channels_first
+
+        def score_head(h, channels_first, p_grouped):
+            qT, kT = channels_first["q"], channels_first["k"]
+
+            def scores(s_acc, i, j):
+                for part in range(2):
+                    nc.tensor.matmul(
+                        out=s_acc,
+                        lhsT=kT[:, part, j * P : (j + 1) * P],
+                        rhs=qT[:, part, i * P : (i + 1) * P],
+                        start=(part == 0),
+                        stop=(part == 1),
+                    )
+
+            def decayed(engine, i, s_tiles):
+                engine.tensor_tensor(
+                    out=p_grouped[:, i * P : (i + 1) * P, 0 : i + 1],
+                    in0=s_tiles.rearrange("p j c -> p c j"),
+                    in1=decay[:, h, :, TILES - 1 - i : TILES],
+                    op=ALU.mult,
+                )
+
+            first_slot = [i * (i + 1) // 2 for i in range(EARLY + 1)]
+            early = psum.tile([P, first_slot[EARLY], P], F32, tag="early")
+            for i in range(EARLY):
+                for j in range(i + 1):
+                    scores(early[:, first_slot[i] + j, :], i, j)
+            early_sb = stage.tile([P, first_slot[EARLY], P], F32)
+            nc.scalar.copy(out=early_sb[:], in_=early[:])
+            for i in range(EARLY):
+                decayed(nc.gpsimd, i, early_sb[:, first_slot[i] : first_slot[i + 1], :])
+            for i in range(EARLY, TILES):
+                late = psum.tile([P, TILES, P], F32, tag="late%d" % (i - EARLY))
+                for j in range(i + 1):
+                    scores(late[:, j, :], i, j)
+                decayed(nc.vector, i, late[:, 0 : i + 1, :])
+
         def project_values(b, h):
-            v_acc = psum.tile([P, TILES, D], F32, tag="quad", bufs=6)
+            v_acc = psum.tile([P, TILES, D], F32, tag="v")
             for j in range(TILES):
                 for g in range(PASSES):
                     nc.tensor.matmul_mx(
@@ -152,67 +228,22 @@ def tile_retention_pb_kernel(
                 in1=bias_all[:, h * D : (h + 1) * D].unsqueeze(2).to_broadcast([P, D, PACK]),
                 op=ALU.add,
             )
+            return v_grouped
+
+        def quantise_head(b, h, p_grouped, v_grouped):
+            p_codes = stage.tile([P, L], U32, align_bytes=64)
+            p_scales = stage.tile([P, L], U8, align_bytes=64)
+            for first in (EARLY * P, 0):
+                cols = slice(first, first + EARLY * P)
+                nc.vector.quantize_mx(
+                    out=p_codes[:, cols].bitcast(FP8X4),
+                    scales=p_scales[:, cols],
+                    in_=p_grouped[:, cols, :].rearrange("p l j -> p (l j)"),
+                )
             nc.vector.quantize_mx(
                 out=v_codes[:, b, h, :].bitcast(FP8X4),
                 scales=v_scales[:, b, h, :],
                 in_=v_grouped[:].rearrange("p d j -> p (d j)"),
-            )
-
-        for n in range(TILES):
-            quantise_rows(x_sb[:, n, :], x_codes[:, n], x_scales[:, n])
-        for n in range(ROW_TILES):
-            quantise_rows(w_sb[:, n, :], w_codes[:, n], w_scales[:, n])
-        for n in range(TILES, ROW_TILES):
-            quantise_rows(x_sb[:, n, :], x_codes[:, n], x_scales[:, n])
-        for b in range(B):
-            for h in range(H):
-                project_values(b, h)
-
-        def flip_head(b, h):
-            channels_first = {}
-            for side in ("q", "k"):
-                flipped = psum.tile([P, 2, L], BF16, tag="flip", bufs=2)
-                for part, name in enumerate((side + "_re", side + "_im")):
-                    resident = rotated[name][0]
-                    for t in range(TILES):
-                        nc.tensor.transpose(
-                            flipped[:, part, t * P : (t + 1) * P],
-                            resident[:, b * TILES + t, h * D : (h + 1) * D],
-                            ident_bf16[:],
-                        )
-                channels_first[side] = stage.tile([P, 2, L], BF16, name=side + "T")
-                if side == "q":
-                    nc.scalar.copy(out=channels_first[side][:], in_=flipped[:])
-                else:
-                    nc.scalar.copy(out=channels_first[side][:, 0, :], in_=flipped[:, 0, :])
-                    nc.scalar.mul(out=channels_first[side][:, 1, :], in_=flipped[:, 1, :], mul=-1.0)
-            return channels_first
-
-        def score_head(h, channels_first, p_grouped):
-            qT, kT = channels_first["q"], channels_first["k"]
-            for i in range(TILES):
-                s_acc = psum.tile([P, TILES, P], F32, tag="quad", bufs=6)
-                for j in range(i + 1):
-                    for part in range(2):
-                        nc.tensor.matmul(
-                            out=s_acc[:, j, :],
-                            lhsT=kT[:, part, j * P : (j + 1) * P],
-                            rhs=qT[:, part, i * P : (i + 1) * P],
-                            start=(part == 0),
-                            stop=(part == 1),
-                        )
-                nc.vector.tensor_tensor(
-                    out=p_grouped[:, i * P : (i + 1) * P, 0 : i + 1],
-                    in0=s_acc[:, 0 : i + 1, :].rearrange("p j c -> p c j"),
-                    in1=decay[:, h, :, TILES - 1 - i : TILES],
-                    op=ALU.mult,
-                )
-            p_codes = stage.tile([P, L], U32, align_bytes=64)
-            p_scales = stage.tile([P, L], U8, align_bytes=64)
-            nc.vector.quantize_mx(
-                out=p_codes[:].bitcast(FP8X4),
-                scales=p_scales[:],
-                in_=p_grouped[:].rearrange("p l j -> p (l j)"),
             )
             return p_codes, p_scales
 
@@ -220,7 +251,7 @@ def tile_retention_pb_kernel(
         results = {}
 
         def attend_head(b, h, p_codes, p_scales):
-            o_acc = psum.tile([P, TILES, D], F32, tag="quad", bufs=6)
+            o_acc = psum.tile([P, TILES, D], F32, tag="o")
             for i in range(TILES):
                 nc.tensor.matmul_mx(
                     out=o_acc[:, i, :],
@@ -231,27 +262,47 @@ def tile_retention_pb_kernel(
                     start=True,
                     stop=True,
                 )
-            member = h % HEAD_GROUP
+            member = h % PAIR
             if member == 0:
-                results["tile"] = stage.tile([P, TILES, HEAD_GROUP, D], F32, name="result", bufs=2)
+                results["tile"] = stage.tile([P, TILES, PAIR, D], F32, name="result")
             result = results["tile"]
             nc.scalar.copy(out=result[:, :, member, :], in_=o_acc[:])
-            if member == HEAD_GROUP - 1:
+            if member == PAIR - 1:
                 first = (h - member) * D
                 nc.sync.dma_start(
-                    out=out_rows[b][:, :, first : first + HEAD_GROUP * D],
+                    out=out_rows[b][:, :, first : first + PAIR * D],
                     in_=result[:].rearrange("p i g d -> p i (g d)"),
                 )
 
-        heads = [(b, h) for b in range(B) for h in range(H)]
-        flipped_of = {}
-        quantised_of = {}
+        def rows_beside(n):
+            b, h = heads[n]
+            if b > 0:
+                return []
+            tiles = [(w_sb[:, h, :], w_codes[:, h], w_scales[:, h])]
+            if h >= TILES:
+                tiles.append((x_sb[:, h, :], x_codes[:, h], x_scales[:, h]))
+            return tiles
+
+        first_x = [flip_rows(x_sb[:, n, :], nc.vector.tensor_copy) for n in range(TILES)]
+        for n in range(TILES):
+            quantise_rows(first_x[n], x_codes[:, n], x_scales[:, n])
+
+        grouped_rows = {}
+        flipped_heads = {}
+        quantised_heads = {}
         for n in range(len(heads) + 2):
             if n < len(heads):
-                flipped_of[n] = flip_head(*heads[n])
+                grouped_rows[n] = [flip_rows(rows[0], nc.scalar.copy) for rows in rows_beside(n)]
+                flipped_heads[n] = flip_head(*heads[n])
+                if heads[n][0] == 0:
+                    build_decay(heads[n][1])
             if 1 <= n <= len(heads):
-                quantised_of[n - 1] = score_head(
-                    heads[n - 1][1], flipped_of[n - 1], p_grouped_ring[(n - 1) % 3]
-                )
+                b, h = heads[n - 1]
+                for grouped, rows in zip(grouped_rows[n - 1], rows_beside(n - 1)):
+                    quantise_rows(grouped, rows[1], rows[2])
+                p_grouped = p_grouped_ring[(n - 1) % 3]
+                score_head(h, flipped_heads[n - 1], p_grouped)
+                v_grouped = project_values(b, h)
+                quantised_heads[n - 1] = quantise_head(b, h, p_grouped, v_grouped)
             if n >= 2:
-                attend_head(*heads[n - 2], *quantised_of[n - 2])
+                attend_head(*heads[n - 2], *quantised_heads[n - 2])

@@ -22,6 +22,7 @@ PASSES = DIM // (P * PACK)
 BANK = 512
 PAIR = 2
 EARLY = 2
+FLIPS_PER_SCORE_TILE = 3
 
 FLOPS = 2 * B * L * DIM * DIM + 2 * B * H * L * L * (2 * D) + 2 * B * H * L * L * D
 
@@ -118,13 +119,6 @@ def tile_retention_pb_kernel(
                 channel_multiplier=-1,
             )
 
-        bias_all = const.tile([P, DIM], BF16)
-        for half in range(DIM // BANK):
-            cols = slice(half * BANK, (half + 1) * BANK)
-            spread = psum.tile([P, BANK], F32, tag="late%d" % half)
-            nc.tensor.matmul(out=spread[:], lhsT=ones[:], rhs=bias_row[:, cols], start=True, stop=True)
-            nc.vector.tensor_copy(out=bias_all[:, cols], in_=spread[:])
-
         x_codes = keep.tile([P, ROW_TILES, PASSES, P], U32, align_bytes=64)
         x_scales = keep.tile([P, ROW_TILES, PASSES, P], U8, align_bytes=64)
         w_codes = keep.tile([P, ROW_TILES, PASSES, P], U32, align_bytes=64)
@@ -152,61 +146,69 @@ def tile_retention_pb_kernel(
                 in_=grouped[:].rearrange("p g r t -> p (g r t)"),
             )
 
-        def flip_head(b, h):
-            channels_first = {}
-            for side in ("q", "k"):
-                flipped = psum.tile([P, 2, L], BF16, tag="flip", bufs=3)
+        def open_flips(b, h):
+            banks = {}
+            flips = []
+            for side in ("k", "q"):
+                banks[side] = psum.tile([P, 2, L], BF16, name="flipped_" + side, tag="flip", bufs=3)
                 for part, name in enumerate((side + "_re", side + "_im")):
                     resident = rotated[name][0]
                     for t in range(TILES):
-                        nc.tensor.transpose(
-                            flipped[:, part, t * P : (t + 1) * P],
-                            resident[:, b * TILES + t, h * D : (h + 1) * D],
-                            ident_bf16[:],
+                        flips.append(
+                            (
+                                banks[side][:, part, t * P : (t + 1) * P],
+                                resident[:, b * TILES + t, h * D : (h + 1) * D],
+                            )
                         )
-                channels_first[side] = stage.tile([P, 2, L], BF16, name=side + "T", bufs=3)
-                if side == "q":
-                    nc.vector.tensor_copy(out=channels_first[side][:], in_=flipped[:])
-                else:
-                    nc.scalar.copy(out=channels_first[side][:, 0, :], in_=flipped[:, 0, :])
-                    nc.scalar.mul(out=channels_first[side][:, 1, :], in_=flipped[:, 1, :], mul=-1.0)
-            return channels_first
+            return banks, flips
 
-        def score_head(h, channels_first, p_grouped):
-            qT, kT = channels_first["q"], channels_first["k"]
+        def transpose_all(flips):
+            for flipped, natural in flips:
+                nc.tensor.transpose(flipped, natural, ident_bf16[:])
 
-            def scores(s_acc, i, j):
+        def close_flips(banks):
+            kT = stage.tile([P, 2, L], BF16, bufs=3)
+            qT = stage.tile([P, 2, L], BF16, bufs=3)
+            nc.scalar.copy(out=kT[:, 0, :], in_=banks["k"][:, 0, :])
+            nc.scalar.mul(out=kT[:, 1, :], in_=banks["k"][:, 1, :], mul=-1.0)
+            nc.vector.tensor_copy(out=qT[:], in_=banks["q"][:])
+            return qT, kT
+
+        def score_tiles(i, s_tiles, qT, kT, flips):
+            for j in range(i + 1):
                 for part in range(2):
                     nc.tensor.matmul(
-                        out=s_acc,
+                        out=s_tiles[:, j, :],
                         lhsT=kT[:, part, j * P : (j + 1) * P],
                         rhs=qT[:, part, i * P : (i + 1) * P],
                         start=(part == 0),
                         stop=(part == 1),
                     )
+                done = (i * (i + 1) // 2 + j) * FLIPS_PER_SCORE_TILE
+                transpose_all(flips[done : done + FLIPS_PER_SCORE_TILE])
 
-            def decayed(engine, i, s_tiles):
-                engine.tensor_tensor(
-                    out=p_grouped[:, i * P : (i + 1) * P, 0 : i + 1],
-                    in0=s_tiles.rearrange("p j c -> p c j"),
-                    in1=decay[:, h, :, TILES - 1 - i : TILES],
-                    op=ALU.mult,
-                )
+        def decayed(engine, h, i, s_tiles, p_grouped):
+            engine.tensor_tensor(
+                out=p_grouped[:, i * P : (i + 1) * P, 0 : i + 1],
+                in0=s_tiles.rearrange("p j c -> p c j"),
+                in1=decay[:, h, :, TILES - 1 - i : TILES],
+                op=ALU.mult,
+            )
 
+        def score_early(h, qT, kT, p_grouped, flips):
             first_slot = [i * (i + 1) // 2 for i in range(EARLY + 1)]
             early = psum.tile([P, first_slot[EARLY], P], F32, tag="early")
             for i in range(EARLY):
-                for j in range(i + 1):
-                    scores(early[:, first_slot[i] + j, :], i, j)
+                score_tiles(i, early[:, first_slot[i] : first_slot[i + 1], :], qT, kT, flips)
             early_sb = stage.tile([P, first_slot[EARLY], P], F32)
             nc.scalar.copy(out=early_sb[:], in_=early[:])
             for i in range(EARLY):
-                decayed(nc.gpsimd, i, early_sb[:, first_slot[i] : first_slot[i + 1], :])
-            for i in range(EARLY, TILES):
-                late = psum.tile([P, TILES, P], F32, tag="late%d" % (i - EARLY))
-                for j in range(i + 1):
-                    scores(late[:, j, :], i, j)
-                decayed(nc.vector, i, late[:, 0 : i + 1, :])
+                decayed(nc.gpsimd, h, i, early_sb[:, first_slot[i] : first_slot[i + 1], :], p_grouped)
+
+        def score_late(h, i, qT, kT, p_grouped, flips):
+            late = psum.tile([P, TILES, P], F32, tag="late%d" % (i - EARLY))
+            score_tiles(i, late[:, 0 : i + 1, :], qT, kT, flips)
+            decayed(nc.vector, h, i, late[:, 0 : i + 1, :], p_grouped)
 
         def project_values(b, h):
             v_acc = psum.tile([P, TILES, D], F32, tag="v")
@@ -287,21 +289,37 @@ def tile_retention_pb_kernel(
         for n in range(TILES):
             quantise_rows(first_x[n], x_codes[:, n], x_scales[:, n])
 
+        bias_all = const.tile([P, DIM], BF16)
+        for half in range(DIM // BANK):
+            cols = slice(half * BANK, (half + 1) * BANK)
+            spread = psum.tile([P, BANK], F32, tag="late%d" % half)
+            nc.tensor.matmul(out=spread[:], lhsT=ones[:], rhs=bias_row[:, cols], start=True, stop=True)
+            nc.vector.tensor_copy(out=bias_all[:, cols], in_=spread[:])
+
         grouped_rows = {}
         flipped_heads = {}
         quantised_heads = {}
         for n in range(len(heads) + 2):
+            banks, flips = None, []
             if n < len(heads):
                 grouped_rows[n] = [flip_rows(rows[0], nc.scalar.copy) for rows in rows_beside(n)]
-                flipped_heads[n] = flip_head(*heads[n])
-                if heads[n][0] == 0:
-                    build_decay(heads[n][1])
+                banks, flips = open_flips(*heads[n])
+            if n == 0:
+                transpose_all(flips)
             if 1 <= n <= len(heads):
                 b, h = heads[n - 1]
                 for grouped, rows in zip(grouped_rows[n - 1], rows_beside(n - 1)):
                     quantise_rows(grouped, rows[1], rows[2])
                 p_grouped = p_grouped_ring[(n - 1) % 3]
-                score_head(h, flipped_heads[n - 1], p_grouped)
+                qT, kT = flipped_heads[n - 1]
+                score_early(h, qT, kT, p_grouped, flips)
+                score_late(h, EARLY, qT, kT, p_grouped, flips)
+            if n < len(heads):
+                flipped_heads[n] = close_flips(banks)
+                if heads[n][0] == 0:
+                    build_decay(heads[n][1])
+            if 1 <= n <= len(heads):
+                score_late(h, EARLY + 1, qT, kT, p_grouped, [])
                 v_grouped = project_values(b, h)
                 quantised_heads[n - 1] = quantise_head(b, h, p_grouped, v_grouped)
             if n >= 2:

@@ -22,7 +22,12 @@ PASSES = DIM // (P * PACK)
 BANK = 512
 PAIR = 2
 EARLY = 2
-FLIPS_PER_SCORE_TILE = 3
+SCORE_TILES = [(i, j) for i in range(TILES) for j in range(i + 1)]
+FLIPS = 2 * 2 * TILES
+FLIPS_PER_SCORE_TILE = 2
+KEYS_FLIPPED = FLIPS // 2 // FLIPS_PER_SCORE_TILE + (FLIPS // 2 % FLIPS_PER_SCORE_TILE > 0) - 1
+QUERIES_FLIPPED = FLIPS // FLIPS_PER_SCORE_TILE + (FLIPS % FLIPS_PER_SCORE_TILE > 0) - 1
+NEVER = 1.0e38
 
 FLOPS = 2 * B * L * DIM * DIM + 2 * B * H * L * L * (2 * D) + 2 * B * H * L * L * D
 
@@ -64,25 +69,28 @@ def tile_retention_pb_kernel(
         w_sb, w_rows = resident_rows("w_sb", wv_w)
         rotated = {}
         for name, tensor in (
-            ("q_re", q_rot_re),
-            ("q_im", q_rot_im),
             ("k_re", k_rot_re),
             ("k_im", k_rot_im),
+            ("q_re", q_rot_re),
+            ("q_im", q_rot_im),
         ):
             rotated[name] = resident_rows(name, tensor.rearrange("b l h d -> (b l) (h d)"))
 
+        for n in range(TILES):
+            nc.sync.dma_start(out=x_sb[:, n, :], in_=x_rows[:, n, :])
         for b in range(B):
-            for n in range(b * TILES, (b + 1) * TILES):
-                nc.sync.dma_start(out=x_sb[:, n, :], in_=x_rows[:, n, :])
-            for first_head in range(0, H, PAIR):
+            for pair in range(H // PAIR):
                 if b == 0:
-                    for n in range(first_head, first_head + PAIR):
+                    for n in range(pair * PAIR, (pair + 1) * PAIR):
                         nc.sync.dma_start(out=w_sb[:, n, :], in_=w_rows[:, n, :])
                 slots = slice(b * TILES, (b + 1) * TILES)
-                cols = slice(first_head * D, (first_head + PAIR) * D)
-                for name in ("q_re", "q_im", "k_re", "k_im"):
+                cols = slice(pair * PAIR * D, (pair + 1) * PAIR * D)
+                for name in ("k_re", "k_im", "q_re", "q_im"):
                     resident, rows = rotated[name]
                     nc.sync.dma_start(out=resident[:, slots, cols], in_=rows[:, slots, cols])
+                if b == 0:
+                    n = TILES + pair
+                    nc.sync.dma_start(out=x_sb[:, n, :], in_=x_rows[:, n, :])
 
         ident_f32 = const.tile([P, P], F32)
         make_identity(nc, ident_f32[:])
@@ -93,30 +101,30 @@ def tile_retention_pb_kernel(
         nc.gpsimd.iota(
             distance_int[:], pattern=distance_pattern, base=farthest, channel_multiplier=-1
         )
-        ident_bf16 = const.tile([P, P], BF16)
-        make_identity(nc, ident_bf16[:])
         distance = const.tile([P, P * TILES], F32)
         nc.vector.tensor_copy(out=distance[:], in_=distance_int[:])
-        nc.vector.tensor_scalar_max(out=distance[:], in0=distance[:], scalar1=0.0)
+        nc.gpsimd.affine_select(
+            out=distance[:],
+            in_=distance[:],
+            pattern=distance_pattern,
+            compare_op=ALU.is_ge,
+            fill=NEVER,
+            base=farthest,
+            channel_multiplier=-1,
+        )
+        ident_bf16 = const.tile([P, P], BF16)
+        make_identity(nc, ident_bf16[:])
 
         log_amp = const.tile([P, H], F32)
         nc.scalar.activation(out=log_amp[:], in_=amplitude_all[:], func=ACT.Sigmoid)
         nc.scalar.activation(out=log_amp[:], in_=log_amp[:], func=ACT.Ln)
+        nc.vector.tensor_scalar_min(out=log_amp[:], in0=log_amp[:], scalar1=-1.0e-30)
         decay = const.tile([P, H, P, TILES], F32)
 
         def build_decay(h):
             decay_h = decay[:, h].rearrange("p c u -> p (c u)")
             nc.scalar.activation(
                 out=decay_h, in_=distance[:], func=ACT.Exp, scale=log_amp[:, h : h + 1]
-            )
-            nc.gpsimd.affine_select(
-                out=decay_h,
-                in_=decay_h,
-                pattern=distance_pattern,
-                compare_op=ALU.is_ge,
-                fill=0.0,
-                base=farthest,
-                channel_multiplier=-1,
             )
 
         x_codes = keep.tile([P, ROW_TILES, PASSES, P], U32, align_bytes=64)
@@ -135,7 +143,7 @@ def tile_retention_pb_kernel(
                     nc.tensor.transpose(
                         flipped[:, g, u, :], words[:, first : first + P], ident_f32[:]
                     )
-            grouped = stage.tile([P, PASSES, P, PACK], BF16, align_bytes=64, bufs=4)
+            grouped = stage.tile([P, PASSES, P, PACK], BF16, align_bytes=64, bufs=5)
             copy(out=grouped[:].bitcast(F32), in_=flipped[:].rearrange("p g u r -> p g r u"))
             return grouped
 
@@ -166,26 +174,16 @@ def tile_retention_pb_kernel(
             for flipped, natural in flips:
                 nc.tensor.transpose(flipped, natural, ident_bf16[:])
 
-        def close_flips(banks):
+        def copy_keys(bank):
             kT = stage.tile([P, 2, L], BF16, bufs=3)
-            qT = stage.tile([P, 2, L], BF16, bufs=3)
-            nc.scalar.copy(out=kT[:, 0, :], in_=banks["k"][:, 0, :])
-            nc.scalar.mul(out=kT[:, 1, :], in_=banks["k"][:, 1, :], mul=-1.0)
-            nc.vector.tensor_copy(out=qT[:], in_=banks["q"][:])
-            return qT, kT
+            nc.scalar.copy(out=kT[:, 0, :], in_=bank[:, 0, :])
+            nc.scalar.mul(out=kT[:, 1, :], in_=bank[:, 1, :], mul=-1.0)
+            return kT
 
-        def score_tiles(i, s_tiles, qT, kT, flips):
-            for j in range(i + 1):
-                for part in range(2):
-                    nc.tensor.matmul(
-                        out=s_tiles[:, j, :],
-                        lhsT=kT[:, part, j * P : (j + 1) * P],
-                        rhs=qT[:, part, i * P : (i + 1) * P],
-                        start=(part == 0),
-                        stop=(part == 1),
-                    )
-                done = (i * (i + 1) // 2 + j) * FLIPS_PER_SCORE_TILE
-                transpose_all(flips[done : done + FLIPS_PER_SCORE_TILE])
+        def copy_queries(bank, copy):
+            qT = stage.tile([P, 2, L], BF16, bufs=3)
+            copy(out=qT[:], in_=bank[:])
+            return qT
 
         def decayed(engine, h, i, s_tiles, p_grouped):
             engine.tensor_tensor(
@@ -195,20 +193,36 @@ def tile_retention_pb_kernel(
                 op=ALU.mult,
             )
 
-        def score_early(h, qT, kT, p_grouped, flips):
-            first_slot = [i * (i + 1) // 2 for i in range(EARLY + 1)]
-            early = psum.tile([P, first_slot[EARLY], P], F32, tag="early")
-            for i in range(EARLY):
-                score_tiles(i, early[:, first_slot[i] : first_slot[i + 1], :], qT, kT, flips)
-            early_sb = stage.tile([P, first_slot[EARLY], P], F32)
-            nc.scalar.copy(out=early_sb[:], in_=early[:])
-            for i in range(EARLY):
-                decayed(nc.gpsimd, h, i, early_sb[:, first_slot[i] : first_slot[i + 1], :], p_grouped)
-
-        def score_late(h, i, qT, kT, p_grouped, flips):
-            late = psum.tile([P, TILES, P], F32, tag="late%d" % (i - EARLY))
-            score_tiles(i, late[:, 0 : i + 1, :], qT, kT, flips)
-            decayed(nc.vector, h, i, late[:, 0 : i + 1, :], p_grouped)
+        def score_head(h, qT, kT, p_grouped, banks, flips, copy):
+            next_qT, next_kT = None, None
+            early = psum.tile([P, EARLY * (EARLY + 1) // 2, P], F32, tag="early")
+            late = None
+            for index, (i, j) in enumerate(SCORE_TILES):
+                if i >= EARLY and j == 0:
+                    late = psum.tile([P, TILES, P], F32, tag="late%d" % (i - EARLY))
+                for part in range(2):
+                    nc.tensor.matmul(
+                        out=early[:, index, :] if i < EARLY else late[:, j, :],
+                        lhsT=kT[:, part, j * P : (j + 1) * P],
+                        rhs=qT[:, part, i * P : (i + 1) * P],
+                        start=(part == 0),
+                        stop=(part == 1),
+                    )
+                done = index * FLIPS_PER_SCORE_TILE
+                transpose_all(flips[done : done + FLIPS_PER_SCORE_TILE])
+                if (i, j) == (EARLY - 1, EARLY - 1):
+                    early_sb = stage.tile([P, EARLY * (EARLY + 1) // 2, P], F32)
+                    nc.scalar.copy(out=early_sb[:], in_=early[:])
+                    for e in range(EARLY):
+                        first = e * (e + 1) // 2
+                        decayed(nc.gpsimd, h, e, early_sb[:, first : first + e + 1, :], p_grouped)
+                if i >= EARLY and j == i:
+                    decayed(nc.vector, h, i, late[:, 0 : i + 1, :], p_grouped)
+                if flips and index == KEYS_FLIPPED:
+                    next_kT = copy_keys(banks["k"])
+                if flips and index == QUERIES_FLIPPED:
+                    next_qT = copy_queries(banks["q"], copy)
+            return next_qT, next_kT
 
         def project_values(b, h):
             v_acc = psum.tile([P, TILES, D], F32, tag="v")
@@ -232,7 +246,7 @@ def tile_retention_pb_kernel(
             )
             return v_grouped
 
-        def quantise_head(b, h, p_grouped, v_grouped):
+        def quantise_p(p_grouped):
             p_codes = stage.tile([P, L], U32, align_bytes=64)
             p_scales = stage.tile([P, L], U8, align_bytes=64)
             for first in (EARLY * P, 0):
@@ -242,12 +256,14 @@ def tile_retention_pb_kernel(
                     scales=p_scales[:, cols],
                     in_=p_grouped[:, cols, :].rearrange("p l j -> p (l j)"),
                 )
+            return p_codes, p_scales
+
+        def quantise_v(b, h, v_grouped):
             nc.vector.quantize_mx(
                 out=v_codes[:, b, h, :].bitcast(FP8X4),
                 scales=v_scales[:, b, h, :],
                 in_=v_grouped[:].rearrange("p d j -> p (d j)"),
             )
-            return p_codes, p_scales
 
         out_rows = out.rearrange("b (i p) c -> b p i c", p=P)
         results = {}
@@ -276,18 +292,18 @@ def tile_retention_pb_kernel(
                     in_=result[:].rearrange("p i g d -> p i (g d)"),
                 )
 
-        def rows_beside(n):
-            b, h = heads[n]
-            if b > 0:
+        def row_tiles(n):
+            if n >= ROW_TILES:
                 return []
-            tiles = [(w_sb[:, h, :], w_codes[:, h], w_scales[:, h])]
-            if h >= TILES:
-                tiles.append((x_sb[:, h, :], x_codes[:, h], x_scales[:, h]))
+            tiles = [(w_sb[:, n, :], w_codes[:, n], w_scales[:, n])]
+            if n >= TILES:
+                tiles.append((x_sb[:, n, :], x_codes[:, n], x_scales[:, n]))
             return tiles
 
-        first_x = [flip_rows(x_sb[:, n, :], nc.vector.tensor_copy) for n in range(TILES)]
-        for n in range(TILES):
-            quantise_rows(first_x[n], x_codes[:, n], x_scales[:, n])
+        first_rows = [(x_sb[:, n, :], x_codes[:, n], x_scales[:, n]) for n in range(TILES)]
+        first_grouped = [flip_rows(rows[0], nc.vector.tensor_copy) for rows in first_rows]
+        for grouped, rows in zip(first_grouped, first_rows):
+            quantise_rows(grouped, rows[1], rows[2])
 
         bias_all = const.tile([P, DIM], BF16)
         for half in range(DIM // BANK):
@@ -296,31 +312,36 @@ def tile_retention_pb_kernel(
             nc.tensor.matmul(out=spread[:], lhsT=ones[:], rhs=bias_row[:, cols], start=True, stop=True)
             nc.vector.tensor_copy(out=bias_all[:, cols], in_=spread[:])
 
+        ahead = 0
         grouped_rows = {}
         flipped_heads = {}
-        quantised_heads = {}
+        quantised_p = {}
         for n in range(len(heads) + 2):
-            banks, flips = None, []
+            grouped_rows[n] = [flip_rows(rows[0], nc.scalar.copy) for rows in row_tiles(n + ahead)]
+            if n >= 1:
+                for grouped, rows in zip(grouped_rows[n - 1], row_tiles(n - 1 + ahead)):
+                    quantise_rows(grouped, rows[1], rows[2])
+            banks, flips, copy = None, [], None
             if n < len(heads):
-                grouped_rows[n] = [flip_rows(rows[0], nc.scalar.copy) for rows in rows_beside(n)]
                 banks, flips = open_flips(*heads[n])
+                copy = nc.vector.tensor_copy
             if n == 0:
                 transpose_all(flips)
+                flipped_heads[n] = (copy_queries(banks["q"], copy), copy_keys(banks["k"]))
             if 1 <= n <= len(heads):
-                b, h = heads[n - 1]
-                for grouped, rows in zip(grouped_rows[n - 1], rows_beside(n - 1)):
-                    quantise_rows(grouped, rows[1], rows[2])
                 p_grouped = p_grouped_ring[(n - 1) % 3]
-                qT, kT = flipped_heads[n - 1]
-                score_early(h, qT, kT, p_grouped, flips)
-                score_late(h, EARLY, qT, kT, p_grouped, flips)
-            if n < len(heads):
-                flipped_heads[n] = close_flips(banks)
-                if heads[n][0] == 0:
-                    build_decay(heads[n][1])
+                flipped_heads[n] = score_head(
+                    heads[n - 1][1], *flipped_heads[n - 1], p_grouped, banks, flips, copy
+                )
+            if n + 0 < H:
+                build_decay(n + 0)
+            projected = n - 1 + ahead
+            v_grouped = None
+            if 0 <= projected < len(heads):
+                v_grouped = project_values(*heads[projected])
             if 1 <= n <= len(heads):
-                score_late(h, EARLY + 1, qT, kT, p_grouped, [])
-                v_grouped = project_values(b, h)
-                quantised_heads[n - 1] = quantise_head(b, h, p_grouped, v_grouped)
+                quantised_p[n - 1] = quantise_p(p_grouped)
+            if 0 <= projected < len(heads):
+                quantise_v(*heads[projected], v_grouped)
             if n >= 2:
-                attend_head(*heads[n - 2], *quantised_heads[n - 2])
+                attend_head(*heads[n - 2], *quantised_p[n - 2])

@@ -23,8 +23,8 @@ BANK = 512
 PAIR = 2
 EARLY = 2
 SCORE_TILES = [(i, j) for i in range(TILES) for j in range(i + 1)]
-FLIPS = 2 * 2 * TILES
-FLIPS_PER_SCORE_TILE = 2
+FLIPS = 2 * TILES
+FLIPS_PER_SCORE_TILE = 4
 KEYS_FLIPPED = FLIPS // 2 // FLIPS_PER_SCORE_TILE + (FLIPS // 2 % FLIPS_PER_SCORE_TILE > 0) - 1
 QUERIES_FLIPPED = FLIPS // FLIPS_PER_SCORE_TILE + (FLIPS % FLIPS_PER_SCORE_TILE > 0) - 1
 NEVER = 1.0e38
@@ -68,29 +68,27 @@ def tile_retention_pb_kernel(
         x_sb, x_rows = resident_rows("x_sb", x.rearrange("b l k -> (b l) k"))
         w_sb, w_rows = resident_rows("w_sb", wv_w)
         rotated = {}
-        for name, tensor in (
-            ("k_re", k_rot_re),
-            ("k_im", k_rot_im),
-            ("q_re", q_rot_re),
-            ("q_im", q_rot_im),
-        ):
-            rotated[name] = resident_rows(name, tensor.rearrange("b l h d -> (b l) (h d)"))
+        for side, parts in (("k", (k_rot_re, k_rot_im)), ("q", (q_rot_re, q_rot_im))):
+            rotated[side] = (
+                inputs.tile([P, B, H, TILES, 2, D], BF16, name=side + "_sb"),
+                [part.rearrange("b (t p) h d -> p (b t) h d", p=P) for part in parts],
+            )
 
         for n in range(TILES):
             nc.sync.dma_start(out=x_sb[:, n, :], in_=x_rows[:, n, :])
         for b in range(B):
-            for pair in range(H // PAIR):
+            slots = slice(b * TILES, (b + 1) * TILES)
+            for h in range(H):
                 if b == 0:
-                    for n in range(pair * PAIR, (pair + 1) * PAIR):
-                        nc.sync.dma_start(out=w_sb[:, n, :], in_=w_rows[:, n, :])
-                slots = slice(b * TILES, (b + 1) * TILES)
-                cols = slice(pair * PAIR * D, (pair + 1) * PAIR * D)
-                for name in ("k_re", "k_im", "q_re", "q_im"):
-                    resident, rows = rotated[name]
-                    nc.sync.dma_start(out=resident[:, slots, cols], in_=rows[:, slots, cols])
-                if b == 0:
-                    n = TILES + pair
-                    nc.sync.dma_start(out=x_sb[:, n, :], in_=x_rows[:, n, :])
+                    nc.sync.dma_start(out=w_sb[:, h, :], in_=w_rows[:, h, :])
+                for side in ("k", "q"):
+                    resident, parts = rotated[side]
+                    for part in range(2):
+                        nc.sync.dma_start(
+                            out=resident[:, b, h, :, part, :], in_=parts[part][:, slots, h, :]
+                        )
+                if b == 0 and h >= TILES:
+                    nc.sync.dma_start(out=x_sb[:, h, :], in_=x_rows[:, h, :])
 
         ident_f32 = const.tile([P, P], F32)
         make_identity(nc, ident_f32[:])
@@ -112,8 +110,6 @@ def tile_retention_pb_kernel(
             base=farthest,
             channel_multiplier=-1,
         )
-        ident_bf16 = const.tile([P, P], BF16)
-        make_identity(nc, ident_bf16[:])
 
         log_amp = const.tile([P, H], F32)
         nc.scalar.activation(out=log_amp[:], in_=amplitude_all[:], func=ACT.Sigmoid)
@@ -154,34 +150,34 @@ def tile_retention_pb_kernel(
                 in_=grouped[:].rearrange("p g r t -> p (g r t)"),
             )
 
+        def negate_imaginary_keys(b, h):
+            k_im = rotated["k"][0][:, b, h, :, 1, :]
+            nc.gpsimd.tensor_scalar(
+                out=k_im, in0=k_im, scalar1=-1.0, scalar2=0.0, op0=ALU.mult, op1=ALU.add
+            )
+
         def open_flips(b, h):
             banks = {}
             flips = []
             for side in ("k", "q"):
-                banks[side] = psum.tile([P, 2, L], BF16, name="flipped_" + side, tag="flip", bufs=3)
-                for part, name in enumerate((side + "_re", side + "_im")):
-                    resident = rotated[name][0]
-                    for t in range(TILES):
-                        flips.append(
-                            (
-                                banks[side][:, part, t * P : (t + 1) * P],
-                                resident[:, b * TILES + t, h * D : (h + 1) * D],
-                            )
-                        )
+                banks[side] = psum.tile([P, L], F32, name="flipped_" + side, tag="flip", bufs=3)
+                resident = rotated[side][0]
+                for t in range(TILES):
+                    words = resident[:, b, h, t].rearrange("p c d -> p (c d)").bitcast(F32)
+                    flips.append((banks[side][:, t * P : (t + 1) * P], words))
             return banks, flips
 
         def transpose_all(flips):
             for flipped, natural in flips:
-                nc.tensor.transpose(flipped, natural, ident_bf16[:])
+                nc.tensor.transpose(flipped, natural, ident_f32[:])
 
         def copy_keys(bank):
-            kT = stage.tile([P, 2, L], BF16, bufs=3)
-            nc.scalar.copy(out=kT[:, 0, :], in_=bank[:, 0, :])
-            nc.scalar.mul(out=kT[:, 1, :], in_=bank[:, 1, :], mul=-1.0)
+            kT = stage.tile([P, L], F32, bufs=3)
+            nc.scalar.copy(out=kT[:], in_=bank[:])
             return kT
 
         def copy_queries(bank, copy):
-            qT = stage.tile([P, 2, L], BF16, bufs=3)
+            qT = stage.tile([P, L], F32, bufs=3)
             copy(out=qT[:], in_=bank[:])
             return qT
 
@@ -195,6 +191,8 @@ def tile_retention_pb_kernel(
 
         def score_head(h, qT, kT, p_grouped, banks, flips, copy):
             next_qT, next_kT = None, None
+            k_halves = kT[:].bitcast(BF16).rearrange("p (l e) -> p l e", e=2)
+            q_halves = qT[:].bitcast(BF16).rearrange("p (l e) -> p l e", e=2)
             early = psum.tile([P, EARLY * (EARLY + 1) // 2, P], F32, tag="early")
             late = None
             for index, (i, j) in enumerate(SCORE_TILES):
@@ -203,8 +201,8 @@ def tile_retention_pb_kernel(
                 for part in range(2):
                     nc.tensor.matmul(
                         out=early[:, index, :] if i < EARLY else late[:, j, :],
-                        lhsT=kT[:, part, j * P : (j + 1) * P],
-                        rhs=qT[:, part, i * P : (i + 1) * P],
+                        lhsT=k_halves[:, j * P : (j + 1) * P, part],
+                        rhs=q_halves[:, i * P : (i + 1) * P, part],
                         start=(part == 0),
                         stop=(part == 1),
                     )
@@ -287,7 +285,7 @@ def tile_retention_pb_kernel(
             nc.scalar.copy(out=result[:, :, member, :], in_=o_acc[:])
             if member == PAIR - 1:
                 first = (h - member) * D
-                nc.sync.dma_start(
+                nc.scalar.dma_start(
                     out=out_rows[b][:, :, first : first + PAIR * D],
                     in_=result[:].rearrange("p i g d -> p i (g d)"),
                 )
@@ -312,6 +310,7 @@ def tile_retention_pb_kernel(
             nc.tensor.matmul(out=spread[:], lhsT=ones[:], rhs=bias_row[:, cols], start=True, stop=True)
             nc.vector.tensor_copy(out=bias_all[:, cols], in_=spread[:])
 
+        negate_imaginary_keys(*heads[0])
         ahead = 0
         grouped_rows = {}
         flipped_heads = {}
@@ -321,10 +320,12 @@ def tile_retention_pb_kernel(
             if n >= 1:
                 for grouped, rows in zip(grouped_rows[n - 1], row_tiles(n - 1 + ahead)):
                     quantise_rows(grouped, rows[1], rows[2])
+            if n + 1 < len(heads):
+                negate_imaginary_keys(*heads[n + 1])
             banks, flips, copy = None, [], None
             if n < len(heads):
                 banks, flips = open_flips(*heads[n])
-                copy = nc.vector.tensor_copy
+                copy = nc.vector.tensor_copy if heads[n][0] == 0 else nc.scalar.copy
             if n == 0:
                 transpose_all(flips)
                 flipped_heads[n] = (copy_queries(banks["q"], copy), copy_keys(banks["k"]))

@@ -20,14 +20,15 @@ TILES = L // P
 ROW_TILES = B * TILES
 PASSES = DIM // (P * PACK)
 BANK = 512
+PARTS = 2
 PAIR = 2
 EARLY = 2
+EARLY_SCORE_TILES = EARLY * (EARLY + 1) // 2
 SCORE_TILES = [(i, j) for i in range(TILES) for j in range(i + 1)]
-FLIPS = 2 * TILES
-FLIPS_PER_SCORE_TILE = 4
-KEYS_FLIPPED = FLIPS // 2 // FLIPS_PER_SCORE_TILE + (FLIPS // 2 % FLIPS_PER_SCORE_TILE > 0) - 1
-QUERIES_FLIPPED = FLIPS // FLIPS_PER_SCORE_TILE + (FLIPS % FLIPS_PER_SCORE_TILE > 0) - 1
+KEYS_FLIPPED = TILES - 1
+QUERIES_FLIPPED = 2 * TILES - 1
 NEVER = 1.0e38
+P_BUFFERS = 3
 
 FLOPS = 2 * B * L * DIM * DIM + 2 * B * H * L * L * (2 * D) + 2 * B * H * L * L * D
 
@@ -54,7 +55,7 @@ def tile_retention_pb_kernel(
         nc.vector.memset(ones[:], 1.0)
 
         p_grouped_ring = []
-        for slot in range(3):
+        for slot in range(P_BUFFERS):
             p_grouped = keep.tile([P, L, PACK], BF16, name="p_grouped%d" % slot, align_bytes=64)
             nc.vector.memset(p_grouped[:].bitcast(I32), 0)
             p_grouped_ring.append(p_grouped)
@@ -68,27 +69,29 @@ def tile_retention_pb_kernel(
         x_sb, x_rows = resident_rows("x_sb", x.rearrange("b l k -> (b l) k"))
         w_sb, w_rows = resident_rows("w_sb", wv_w)
         rotated = {}
-        for side, parts in (("k", (k_rot_re, k_rot_im)), ("q", (q_rot_re, q_rot_im))):
-            rotated[side] = (
-                inputs.tile([P, B, H, TILES, 2, D], BF16, name=side + "_sb"),
-                [part.rearrange("b (t p) h d -> p (b t) h d", p=P) for part in parts],
-            )
+        for name, tensor in (
+            ("k_re", k_rot_re),
+            ("k_im", k_rot_im),
+            ("q_re", q_rot_re),
+            ("q_im", q_rot_im),
+        ):
+            rotated[name] = resident_rows(name, tensor.rearrange("b l h d -> (b l) (h d)"))
 
         for n in range(TILES):
             nc.sync.dma_start(out=x_sb[:, n, :], in_=x_rows[:, n, :])
         for b in range(B):
-            slots = slice(b * TILES, (b + 1) * TILES)
-            for h in range(H):
+            for pair in range(H // PAIR):
                 if b == 0:
-                    nc.sync.dma_start(out=w_sb[:, h, :], in_=w_rows[:, h, :])
-                for side in ("k", "q"):
-                    resident, parts = rotated[side]
-                    for part in range(2):
-                        nc.sync.dma_start(
-                            out=resident[:, b, h, :, part, :], in_=parts[part][:, slots, h, :]
-                        )
-                if b == 0 and h >= TILES:
-                    nc.sync.dma_start(out=x_sb[:, h, :], in_=x_rows[:, h, :])
+                    for n in range(pair * PAIR, (pair + 1) * PAIR):
+                        nc.sync.dma_start(out=w_sb[:, n, :], in_=w_rows[:, n, :])
+                slots = slice(b * TILES, (b + 1) * TILES)
+                cols = slice(pair * PAIR * D, (pair + 1) * PAIR * D)
+                for name in ("k_re", "k_im", "q_re", "q_im"):
+                    resident, rows = rotated[name]
+                    nc.sync.dma_start(out=resident[:, slots, cols], in_=rows[:, slots, cols])
+                if b == 0:
+                    n = TILES + pair
+                    nc.sync.dma_start(out=x_sb[:, n, :], in_=x_rows[:, n, :])
 
         ident_f32 = const.tile([P, P], F32)
         make_identity(nc, ident_f32[:])
@@ -110,6 +113,8 @@ def tile_retention_pb_kernel(
             base=farthest,
             channel_multiplier=-1,
         )
+        ident_bf16 = const.tile([P, P], BF16)
+        make_identity(nc, ident_bf16[:])
 
         log_amp = const.tile([P, H], F32)
         nc.scalar.activation(out=log_amp[:], in_=amplitude_all[:], func=ACT.Sigmoid)
@@ -118,9 +123,11 @@ def tile_retention_pb_kernel(
         decay = const.tile([P, H, P, TILES], F32)
 
         def build_decay(h):
-            decay_h = decay[:, h].rearrange("p c u -> p (c u)")
             nc.scalar.activation(
-                out=decay_h, in_=distance[:], func=ACT.Exp, scale=log_amp[:, h : h + 1]
+                out=decay[:, h].rearrange("p c u -> p (c u)"),
+                in_=distance[:],
+                func=ACT.Exp,
+                scale=log_amp[:, h : h + 1],
             )
 
         x_codes = keep.tile([P, ROW_TILES, PASSES, P], U32, align_bytes=64)
@@ -150,35 +157,37 @@ def tile_retention_pb_kernel(
                 in_=grouped[:].rearrange("p g r t -> p (g r t)"),
             )
 
-        def negate_imaginary_keys(b, h):
-            k_im = rotated["k"][0][:, b, h, :, 1, :]
-            nc.gpsimd.tensor_scalar(
-                out=k_im, in0=k_im, scalar1=-1.0, scalar2=0.0, op0=ALU.mult, op1=ALU.add
-            )
-
         def open_flips(b, h):
             banks = {}
             flips = []
             for side in ("k", "q"):
-                banks[side] = psum.tile([P, L], F32, name="flipped_" + side, tag="flip", bufs=3)
-                resident = rotated[side][0]
-                for t in range(TILES):
-                    words = resident[:, b, h, t].rearrange("p c d -> p (c d)").bitcast(F32)
-                    flips.append((banks[side][:, t * P : (t + 1) * P], words))
+                banks[side] = psum.tile(
+                    [P, PARTS, L], BF16, name="flipped_" + side, tag="flip", bufs=3
+                )
+                for part, name in enumerate((side + "_re", side + "_im")):
+                    resident = rotated[name][0]
+                    for t in range(TILES):
+                        flips.append(
+                            (
+                                banks[side][:, part, t * P : (t + 1) * P],
+                                resident[:, b * TILES + t, h * D : (h + 1) * D],
+                            )
+                        )
             return banks, flips
 
         def transpose_all(flips):
             for flipped, natural in flips:
-                nc.tensor.transpose(flipped, natural, ident_f32[:])
+                nc.tensor.transpose(flipped, natural, ident_bf16[:])
 
         def copy_keys(bank):
-            kT = stage.tile([P, L], F32, bufs=3)
-            nc.scalar.copy(out=kT[:], in_=bank[:])
+            kT = stage.tile([P, PARTS, L], BF16, bufs=3)
+            nc.scalar.copy(out=kT[:, 0, :], in_=bank[:, 0, :])
+            nc.scalar.mul(out=kT[:, 1, :], in_=bank[:, 1, :], mul=-1.0)
             return kT
 
-        def copy_queries(bank, copy):
-            qT = stage.tile([P, L], F32, bufs=3)
-            copy(out=qT[:], in_=bank[:])
+        def copy_queries(bank):
+            qT = stage.tile([P, PARTS, L], BF16, bufs=3)
+            nc.vector.tensor_copy(out=qT[:], in_=bank[:])
             return qT
 
         def decayed(engine, h, i, s_tiles, p_grouped):
@@ -189,27 +198,24 @@ def tile_retention_pb_kernel(
                 op=ALU.mult,
             )
 
-        def score_head(h, qT, kT, p_grouped, banks, flips, copy):
+        def score_head(h, qT, kT, p_grouped, banks, flips):
             next_qT, next_kT = None, None
-            k_halves = kT[:].bitcast(BF16).rearrange("p (l e) -> p l e", e=2)
-            q_halves = qT[:].bitcast(BF16).rearrange("p (l e) -> p l e", e=2)
-            early = psum.tile([P, EARLY * (EARLY + 1) // 2, P], F32, tag="early")
+            early = psum.tile([P, EARLY_SCORE_TILES, P], F32, tag="early")
             late = None
             for index, (i, j) in enumerate(SCORE_TILES):
                 if i >= EARLY and j == 0:
                     late = psum.tile([P, TILES, P], F32, tag="late%d" % (i - EARLY))
-                for part in range(2):
+                for part in range(PARTS):
                     nc.tensor.matmul(
                         out=early[:, index, :] if i < EARLY else late[:, j, :],
-                        lhsT=k_halves[:, j * P : (j + 1) * P, part],
-                        rhs=q_halves[:, i * P : (i + 1) * P, part],
+                        lhsT=kT[:, part, j * P : (j + 1) * P],
+                        rhs=qT[:, part, i * P : (i + 1) * P],
                         start=(part == 0),
-                        stop=(part == 1),
+                        stop=(part == PARTS - 1),
                     )
-                done = index * FLIPS_PER_SCORE_TILE
-                transpose_all(flips[done : done + FLIPS_PER_SCORE_TILE])
+                    transpose_all(flips[PARTS * index + part : PARTS * index + part + 1])
                 if (i, j) == (EARLY - 1, EARLY - 1):
-                    early_sb = stage.tile([P, EARLY * (EARLY + 1) // 2, P], F32)
+                    early_sb = stage.tile([P, EARLY_SCORE_TILES, P], F32)
                     nc.scalar.copy(out=early_sb[:], in_=early[:])
                     for e in range(EARLY):
                         first = e * (e + 1) // 2
@@ -219,7 +225,7 @@ def tile_retention_pb_kernel(
                 if flips and index == KEYS_FLIPPED:
                     next_kT = copy_keys(banks["k"])
                 if flips and index == QUERIES_FLIPPED:
-                    next_qT = copy_queries(banks["q"], copy)
+                    next_qT = copy_queries(banks["q"])
             return next_qT, next_kT
 
         def project_values(b, h):
@@ -285,7 +291,7 @@ def tile_retention_pb_kernel(
             nc.scalar.copy(out=result[:, :, member, :], in_=o_acc[:])
             if member == PAIR - 1:
                 first = (h - member) * D
-                nc.scalar.dma_start(
+                nc.sync.dma_start(
                     out=out_rows[b][:, :, first : first + PAIR * D],
                     in_=result[:].rearrange("p i g d -> p i (g d)"),
                 )
@@ -310,39 +316,27 @@ def tile_retention_pb_kernel(
             nc.tensor.matmul(out=spread[:], lhsT=ones[:], rhs=bias_row[:, cols], start=True, stop=True)
             nc.vector.tensor_copy(out=bias_all[:, cols], in_=spread[:])
 
-        negate_imaginary_keys(*heads[0])
-        ahead = 0
         grouped_rows = {}
         flipped_heads = {}
         quantised_p = {}
         for n in range(len(heads) + 2):
-            grouped_rows[n] = [flip_rows(rows[0], nc.scalar.copy) for rows in row_tiles(n + ahead)]
+            grouped_rows[n] = [flip_rows(rows[0], nc.scalar.copy) for rows in row_tiles(n)]
             if n >= 1:
-                for grouped, rows in zip(grouped_rows[n - 1], row_tiles(n - 1 + ahead)):
+                for grouped, rows in zip(grouped_rows[n - 1], row_tiles(n - 1)):
                     quantise_rows(grouped, rows[1], rows[2])
-            if n + 1 < len(heads):
-                negate_imaginary_keys(*heads[n + 1])
-            banks, flips, copy = None, [], None
-            if n < len(heads):
-                banks, flips = open_flips(*heads[n])
-                copy = nc.vector.tensor_copy if heads[n][0] == 0 else nc.scalar.copy
+            banks, flips = open_flips(*heads[n]) if n < len(heads) else (None, [])
             if n == 0:
                 transpose_all(flips)
-                flipped_heads[n] = (copy_queries(banks["q"], copy), copy_keys(banks["k"]))
+                flipped_heads[n] = (copy_queries(banks["q"]), copy_keys(banks["k"]))
             if 1 <= n <= len(heads):
-                p_grouped = p_grouped_ring[(n - 1) % 3]
-                flipped_heads[n] = score_head(
-                    heads[n - 1][1], *flipped_heads[n - 1], p_grouped, banks, flips, copy
-                )
-            if n + 0 < H:
-                build_decay(n + 0)
-            projected = n - 1 + ahead
-            v_grouped = None
-            if 0 <= projected < len(heads):
-                v_grouped = project_values(*heads[projected])
+                b, h = heads[n - 1]
+                p_grouped = p_grouped_ring[(n - 1) % P_BUFFERS]
+                flipped_heads[n] = score_head(h, *flipped_heads[n - 1], p_grouped, banks, flips)
+            if n < H:
+                build_decay(n)
             if 1 <= n <= len(heads):
+                v_grouped = project_values(b, h)
                 quantised_p[n - 1] = quantise_p(p_grouped)
-            if 0 <= projected < len(heads):
-                quantise_v(*heads[projected], v_grouped)
+                quantise_v(b, h, v_grouped)
             if n >= 2:
                 attend_head(*heads[n - 2], *quantised_p[n - 2])

@@ -115,6 +115,8 @@ def tile_retention_pb_kernel(
         )
         ident_bf16 = const.tile([P, P], BF16)
         make_identity(nc, ident_bf16[:])
+        minus_ident = const.tile([P, P], BF16)
+        nc.vector.tensor_scalar_mul(out=minus_ident[:], in0=ident_bf16[:], scalar1=-1.0)
 
         log_amp = const.tile([P, H], F32)
         nc.scalar.activation(out=log_amp[:], in_=amplitude_all[:], func=ACT.Sigmoid)
@@ -171,23 +173,28 @@ def tile_retention_pb_kernel(
                             (
                                 banks[side][:, part, t * P : (t + 1) * P],
                                 resident[:, b * TILES + t, h * D : (h + 1) * D],
+                                name == "k_im",
                             )
                         )
             return banks, flips
 
         def transpose_all(flips):
-            for flipped, natural in flips:
-                nc.tensor.transpose(flipped, natural, ident_bf16[:])
+            for flipped, natural, negate in flips:
+                if negate:
+                    nc.tensor.matmul(
+                        out=flipped, lhsT=natural, rhs=minus_ident[:], start=True, stop=True
+                    )
+                else:
+                    nc.tensor.transpose(flipped, natural, ident_bf16[:])
 
         def copy_keys(bank):
             kT = stage.tile([P, PARTS, L], BF16, bufs=3)
-            nc.scalar.copy(out=kT[:, 0, :], in_=bank[:, 0, :])
-            nc.scalar.mul(out=kT[:, 1, :], in_=bank[:, 1, :], mul=-1.0)
+            nc.scalar.copy(out=kT[:], in_=bank[:])
             return kT
 
         def copy_queries(bank):
             qT = stage.tile([P, PARTS, L], BF16, bufs=3)
-            nc.vector.tensor_copy(out=qT[:], in_=bank[:])
+            nc.scalar.copy(out=qT[:], in_=bank[:])
             return qT
 
         def decayed(engine, h, i, s_tiles, p_grouped):

@@ -192,9 +192,9 @@ def tile_retention_pb_kernel(
             nc.scalar.copy(out=kT[:], in_=bank[:])
             return kT
 
-        def copy_queries(bank):
+        def copy_queries(bank, copy):
             qT = stage.tile([P, PARTS, L], BF16, bufs=3)
-            nc.scalar.copy(out=qT[:], in_=bank[:])
+            copy(out=qT[:], in_=bank[:])
             return qT
 
         def decayed(engine, h, i, s_tiles, p_grouped):
@@ -205,7 +205,7 @@ def tile_retention_pb_kernel(
                 op=ALU.mult,
             )
 
-        def score_head(h, qT, kT, p_grouped, banks, flips):
+        def score_head(h, qT, kT, p_grouped, banks, flips, q_copy):
             next_qT, next_kT = None, None
             early = psum.tile([P, EARLY_SCORE_TILES, P], F32, tag="early")
             late = None
@@ -232,7 +232,7 @@ def tile_retention_pb_kernel(
                 if flips and index == KEYS_FLIPPED:
                     next_kT = copy_keys(banks["k"])
                 if flips and index == QUERIES_FLIPPED:
-                    next_qT = copy_queries(banks["q"])
+                    next_qT = copy_queries(banks["q"], q_copy)
             return next_qT, next_kT
 
         def project_values(b, h):
@@ -293,7 +293,7 @@ def tile_retention_pb_kernel(
                 )
             member = h % PAIR
             if member == 0:
-                results["tile"] = stage.tile([P, TILES, PAIR, D], F32, name="result")
+                results["tile"] = stage.tile([P, TILES, PAIR, D], F32, name="result", bufs=4)
             result = results["tile"]
             nc.scalar.copy(out=result[:, :, member, :], in_=o_acc[:])
             if member == PAIR - 1:
@@ -334,11 +334,11 @@ def tile_retention_pb_kernel(
             banks, flips = open_flips(*heads[n]) if n < len(heads) else (None, [])
             if n == 0:
                 transpose_all(flips)
-                flipped_heads[n] = (copy_queries(banks["q"]), copy_keys(banks["k"]))
+                flipped_heads[n] = (copy_queries(banks["q"], nc.vector.tensor_copy), copy_keys(banks["k"]))
             if 1 <= n <= len(heads):
                 b, h = heads[n - 1]
                 p_grouped = p_grouped_ring[(n - 1) % P_BUFFERS]
-                flipped_heads[n] = score_head(h, *flipped_heads[n - 1], p_grouped, banks, flips)
+                flipped_heads[n] = score_head(h, *flipped_heads[n - 1], p_grouped, banks, flips, nc.vector.tensor_copy if n < H else nc.scalar.copy)
             if n < H:
                 build_decay(n)
             if 1 <= n <= len(heads):

@@ -28,6 +28,7 @@ SCORE_TILES = [(i, j) for i in range(TILES) for j in range(i + 1)]
 KEYS_FLIPPED = TILES - 1
 QUERIES_FLIPPED = 2 * TILES - 1
 NEVER = 1.0e38
+RESULT_BUFFERS = 6
 P_BUFFERS = 3
 
 FLOPS = 2 * B * L * DIM * DIM + 2 * B * H * L * L * (2 * D) + 2 * B * H * L * L * D
@@ -46,11 +47,8 @@ def tile_retention_pb_kernel(
         stage = ctx.enter_context(tc.tile_pool(name="stage", bufs=2))
         psum = ctx.enter_context(tc.psum_pool(name="psum", bufs=1))
 
-        amplitude_all = const.tile([P, H], BF16)
-        nc.scalar.dma_start(out=amplitude_all[:], in_=amplitude.partition_broadcast(P))
-        bias_row = const.tile([P, DIM], BF16)
-        nc.vector.memset(bias_row[:].bitcast(I32), 0)
-        nc.scalar.dma_start(out=bias_row[0:1, :], in_=wv_b.rearrange("(o c) -> o c", o=1))
+        small_row = const.tile([P, DIM + H], BF16)
+        nc.vector.memset(small_row[:].bitcast(I32), 0)
         ones = const.tile([P, P], BF16)
         nc.vector.memset(ones[:], 1.0)
 
@@ -77,22 +75,35 @@ def tile_retention_pb_kernel(
         ):
             rotated[name] = resident_rows(name, tensor.rearrange("b l h d -> (b l) (h d)"))
 
-        for n in range(TILES):
-            nc.sync.dma_start(out=x_sb[:, n, :], in_=x_rows[:, n, :])
-        for b in range(B):
-            for pair in range(H // PAIR):
-                if b == 0:
-                    for n in range(pair * PAIR, (pair + 1) * PAIR):
-                        nc.sync.dma_start(out=w_sb[:, n, :], in_=w_rows[:, n, :])
-                slots = slice(b * TILES, (b + 1) * TILES)
-                cols = slice(pair * PAIR * D, (pair + 1) * PAIR * D)
-                for name in ("k_re", "k_im", "q_re", "q_im"):
-                    resident, rows = rotated[name]
-                    nc.sync.dma_start(out=resident[:, slots, cols], in_=rows[:, slots, cols])
-                if b == 0:
-                    n = TILES + pair
-                    nc.sync.dma_start(out=x_sb[:, n, :], in_=x_rows[:, n, :])
+        def load_heads(b, first, count, names=("k_re", "k_im", "q_re", "q_im")):
+            slots = slice(b * TILES, (b + 1) * TILES)
+            cols = slice(first * D, (first + count) * D)
+            for name in names:
+                resident, rows = rotated[name]
+                nc.sync.dma_start(out=resident[:, slots, cols], in_=rows[:, slots, cols])
 
+        def load_rows(resident, rows, tiles):
+            for n in tiles:
+                nc.sync.dma_start(out=resident[:, n, :], in_=rows[:, n, :])
+
+        load_heads(0, 0, PAIR, ("k_re", "k_im"))
+        nc.sync.dma_start(out=small_row[0:1, DIM:], in_=amplitude.rearrange("(o c) -> o c", o=1))
+        nc.sync.dma_start(out=small_row[0:1, :DIM], in_=wv_b.rearrange("(o c) -> o c", o=1))
+        load_heads(0, 0, PAIR, ("q_re", "q_im"))
+        load_rows(x_sb, x_rows, range(TILES))
+        for pair in range(1, H // PAIR):
+            load_rows(w_sb, w_rows, range(2 * pair - 2, 2 * pair))
+            load_heads(0, pair * PAIR, PAIR)
+            load_rows(x_sb, x_rows, range(TILES + pair - 1, TILES + pair))
+        load_rows(w_sb, w_rows, range(6, 8))
+        load_rows(x_sb, x_rows, range(7, 8))
+        for pair in range(H // PAIR):
+            load_heads(1, pair * PAIR, PAIR)
+
+        ident_bf16 = const.tile([P, P], BF16)
+        make_identity(nc, ident_bf16[:])
+        minus_ident = const.tile([P, P], BF16)
+        nc.vector.tensor_scalar_mul(out=minus_ident[:], in0=ident_bf16[:], scalar1=-1.0)
         ident_f32 = const.tile([P, P], F32)
         make_identity(nc, ident_f32[:])
 
@@ -113,15 +124,8 @@ def tile_retention_pb_kernel(
             base=farthest,
             channel_multiplier=-1,
         )
-        ident_bf16 = const.tile([P, P], BF16)
-        make_identity(nc, ident_bf16[:])
-        minus_ident = const.tile([P, P], BF16)
-        nc.vector.tensor_scalar_mul(out=minus_ident[:], in0=ident_bf16[:], scalar1=-1.0)
 
         log_amp = const.tile([P, H], F32)
-        nc.scalar.activation(out=log_amp[:], in_=amplitude_all[:], func=ACT.Sigmoid)
-        nc.scalar.activation(out=log_amp[:], in_=log_amp[:], func=ACT.Ln)
-        nc.vector.tensor_scalar_min(out=log_amp[:], in0=log_amp[:], scalar1=-1.0e-30)
         decay = const.tile([P, H, P, TILES], F32)
 
         def build_decay(h):
@@ -139,18 +143,29 @@ def tile_retention_pb_kernel(
         v_codes = keep.tile([P, B, H, D], U32, align_bytes=64)
         v_scales = keep.tile([P, B, H, D], U8, align_bytes=64)
 
-        def flip_rows(rows_sb, copy):
+        flipped = {}
+        pending_rows = []
+
+        def row_steps(rows_sb, codes, scales, copy):
             words = rows_sb.bitcast(F32)
-            flipped = psum.tile([P, PASSES, 2, P], F32, tag="flip", bufs=3)
-            for g in range(PASSES):
-                for u in range(2):
-                    first = (2 * g + u) * P
-                    nc.tensor.transpose(
-                        flipped[:, g, u, :], words[:, first : first + P], ident_f32[:]
+            box = {}
+
+            def step(g, u):
+                if (g, u) == (0, 0):
+                    box["bank"] = psum.tile([P, PASSES, 2, P], F32, name="flip_rows", tag="flip", bufs=3)
+                first = (2 * g + u) * P
+                nc.tensor.transpose(
+                    box["bank"][:, g, u, :], words[:, first : first + P], ident_f32[:]
+                )
+                if (g, u) == (PASSES - 1, 1):
+                    grouped = stage.tile([P, PASSES, P, PACK], BF16, align_bytes=64, bufs=5)
+                    copy(
+                        out=grouped[:].bitcast(F32),
+                        in_=box["bank"][:].rearrange("p g u r -> p g r u"),
                     )
-            grouped = stage.tile([P, PASSES, P, PACK], BF16, align_bytes=64, bufs=5)
-            copy(out=grouped[:].bitcast(F32), in_=flipped[:].rearrange("p g u r -> p g r u"))
-            return grouped
+                    pending_rows.append((grouped, codes, scales))
+
+            return [lambda g=g, u=u: step(g, u) for g in range(PASSES) for u in range(2)]
 
         def quantise_rows(grouped, codes, scales):
             nc.vector.quantize_mx(
@@ -159,43 +174,49 @@ def tile_retention_pb_kernel(
                 in_=grouped[:].rearrange("p g r t -> p (g r t)"),
             )
 
-        def open_flips(b, h):
-            banks = {}
-            flips = []
-            for side in ("k", "q"):
-                banks[side] = psum.tile(
-                    [P, PARTS, L], BF16, name="flipped_" + side, tag="flip", bufs=3
-                )
-                for part, name in enumerate((side + "_re", side + "_im")):
-                    resident = rotated[name][0]
-                    for t in range(TILES):
-                        flips.append(
-                            (
-                                banks[side][:, part, t * P : (t + 1) * P],
-                                resident[:, b * TILES + t, h * D : (h + 1) * D],
-                                name == "k_im",
-                            )
-                        )
-            return banks, flips
+        def quantise_pending():
+            for grouped, codes, scales in pending_rows:
+                quantise_rows(grouped, codes, scales)
+            pending_rows.clear()
 
-        def transpose_all(flips):
-            for flipped, natural, negate in flips:
-                if negate:
+        def head_steps(n, k_copy, q_copy, by_part):
+            b, h = heads[n]
+            flipped[n] = {}
+
+            def step(side, part, t, copy):
+                if t == 0 and (by_part or part == 0):
+                    flipped[n][side + "_bank"] = psum.tile(
+                        [P, PARTS, L], BF16, name="flipped_" + side, tag="flip", bufs=3
+                    )
+                bank = flipped[n][side + "_bank"]
+                name = side + ("_re", "_im")[part]
+                target = bank[:, part, t * P : (t + 1) * P]
+                natural = rotated[name][0][:, b * TILES + t, h * D : (h + 1) * D]
+                if name == "k_im":
                     nc.tensor.matmul(
-                        out=flipped, lhsT=natural, rhs=minus_ident[:], start=True, stop=True
+                        out=target, lhsT=natural, rhs=minus_ident[:], start=True, stop=True
                     )
                 else:
-                    nc.tensor.transpose(flipped, natural, ident_bf16[:])
+                    nc.tensor.transpose(target, natural, ident_bf16[:])
+                if t == TILES - 1 and (by_part or part == PARTS - 1):
+                    if by_part:
+                        if part == 0:
+                            flipped[n][side] = stage.tile([P, PARTS, L], BF16, name=side + "T", bufs=3)
+                        copy(out=flipped[n][side][:, part, :], in_=bank[:, part, :])
+                    else:
+                        flipped[n][side] = stage.tile([P, PARTS, L], BF16, name=side + "T", bufs=3)
+                        copy(out=flipped[n][side][:], in_=bank[:])
 
-        def copy_keys(bank):
-            kT = stage.tile([P, PARTS, L], BF16, bufs=3)
-            nc.scalar.copy(out=kT[:], in_=bank[:])
-            return kT
+            return [
+                lambda side=side, part=part, t=t, copy=copy: step(side, part, t, copy)
+                for side, copy in (("k", k_copy), ("q", q_copy))
+                for part in range(PARTS)
+                for t in range(TILES)
+            ]
 
-        def copy_queries(bank, copy):
-            qT = stage.tile([P, PARTS, L], BF16, bufs=3)
-            copy(out=qT[:], in_=bank[:])
-            return qT
+        def run(steps):
+            for step in steps:
+                step()
 
         def decayed(engine, h, i, s_tiles, p_grouped):
             engine.tensor_tensor(
@@ -205,8 +226,11 @@ def tile_retention_pb_kernel(
                 op=ALU.mult,
             )
 
-        def score_head(h, qT, kT, p_grouped, banks, flips, q_copy):
-            next_qT, next_kT = None, None
+        def score_head(n, steps, between):
+            h = heads[n][1]
+            qT, kT = flipped[n]["q"], flipped[n]["k"]
+            p_grouped = p_grouped_ring[n % P_BUFFERS]
+            steps = list(steps)
             early = psum.tile([P, EARLY_SCORE_TILES, P], F32, tag="early")
             late = None
             for index, (i, j) in enumerate(SCORE_TILES):
@@ -220,23 +244,23 @@ def tile_retention_pb_kernel(
                         start=(part == 0),
                         stop=(part == PARTS - 1),
                     )
-                    transpose_all(flips[PARTS * index + part : PARTS * index + part + 1])
+                    run(steps[:1])
+                    steps = steps[1:]
                 if (i, j) == (EARLY - 1, EARLY - 1):
                     early_sb = stage.tile([P, EARLY_SCORE_TILES, P], F32)
                     nc.scalar.copy(out=early_sb[:], in_=early[:])
+                    for m in between:
+                        quantise_v(m, project_values(m))
                     for e in range(EARLY):
                         first = e * (e + 1) // 2
                         decayed(nc.gpsimd, h, e, early_sb[:, first : first + e + 1, :], p_grouped)
                 if i >= EARLY and j == i:
                     decayed(nc.vector, h, i, late[:, 0 : i + 1, :], p_grouped)
-                if flips and index == KEYS_FLIPPED:
-                    next_kT = copy_keys(banks["k"])
-                if flips and index == QUERIES_FLIPPED:
-                    next_qT = copy_queries(banks["q"], q_copy)
-            return next_qT, next_kT
+            run(steps)
 
-        def project_values(b, h):
-            v_acc = psum.tile([P, TILES, D], F32, tag="v")
+        def project_values(n):
+            b, h = heads[n]
+            v_acc = psum.tile([P, TILES, D], F32, tag="mx", bufs=2)
             for j in range(TILES):
                 for g in range(PASSES):
                     nc.tensor.matmul_mx(
@@ -257,9 +281,10 @@ def tile_retention_pb_kernel(
             )
             return v_grouped
 
-        def quantise_p(p_grouped):
-            p_codes = stage.tile([P, L], U32, align_bytes=64)
-            p_scales = stage.tile([P, L], U8, align_bytes=64)
+        def quantise_p(n):
+            p_grouped = p_grouped_ring[n % P_BUFFERS]
+            p_codes = stage.tile([P, L], U32, align_bytes=64, bufs=4)
+            p_scales = stage.tile([P, L], U8, align_bytes=64, bufs=4)
             for first in (EARLY * P, 0):
                 cols = slice(first, first + EARLY * P)
                 nc.vector.quantize_mx(
@@ -267,9 +292,10 @@ def tile_retention_pb_kernel(
                     scales=p_scales[:, cols],
                     in_=p_grouped[:, cols, :].rearrange("p l j -> p (l j)"),
                 )
-            return p_codes, p_scales
+            quantised_p[n] = (p_codes, p_scales)
 
-        def quantise_v(b, h, v_grouped):
+        def quantise_v(n, v_grouped):
+            b, h = heads[n]
             nc.vector.quantize_mx(
                 out=v_codes[:, b, h, :].bitcast(FP8X4),
                 scales=v_scales[:, b, h, :],
@@ -279,11 +305,13 @@ def tile_retention_pb_kernel(
         out_rows = out.rearrange("b (i p) c -> b p i c", p=P)
         results = {}
 
-        def attend_head(b, h, p_codes, p_scales):
-            o_acc = psum.tile([P, TILES, D], F32, tag="o")
-            for i in range(TILES):
+        def attend_tiles(n, tiles):
+            b, h = heads[n]
+            p_codes, p_scales = quantised_p[n]
+            o_acc = psum.tile([P, len(tiles), D], F32, name="o_acc", tag="mx", bufs=2)
+            for place, i in enumerate(tiles):
                 nc.tensor.matmul_mx(
-                    out=o_acc[:, i, :],
+                    out=o_acc[:, place, :],
                     lhsT=p_codes[:, i * P : (i + 1) * P].bitcast(FP8X4),
                     lhsT_scale=p_scales[:, i * P : (i + 1) * P],
                     rhs=v_codes[:, b, h, :].bitcast(FP8X4),
@@ -291,59 +319,94 @@ def tile_retention_pb_kernel(
                     start=True,
                     stop=True,
                 )
+            return o_acc
+
+        def attend_head(n):
+            b, h = heads[n]
+            o_acc = attend_tiles(n, range(TILES))
             member = h % PAIR
             if member == 0:
-                results["tile"] = stage.tile([P, TILES, PAIR, D], F32, name="result", bufs=4)
+                results["tile"] = stage.tile([P, TILES, PAIR, D], F32, name="result", bufs=RESULT_BUFFERS)
             result = results["tile"]
             nc.scalar.copy(out=result[:, :, member, :], in_=o_acc[:])
-            if member == PAIR - 1:
+            if n == len(heads) - 2:
+                nc.sync.dma_start(
+                    out=out_rows[b][:, :, h * D : (h + 1) * D], in_=result[:, :, member, :]
+                )
+            elif member == PAIR - 1:
                 first = (h - member) * D
                 nc.sync.dma_start(
                     out=out_rows[b][:, :, first : first + PAIR * D],
                     in_=result[:].rearrange("p i g d -> p i (g d)"),
                 )
 
-        def row_tiles(n):
-            if n >= ROW_TILES:
-                return []
-            tiles = [(w_sb[:, n, :], w_codes[:, n], w_scales[:, n])]
-            if n >= TILES:
-                tiles.append((x_sb[:, n, :], x_codes[:, n], x_scales[:, n]))
-            return tiles
+        def attend_last_head(n):
+            b, h = heads[n]
+            for first, copy, queue in (
+                (EARLY, nc.scalar.copy, nc.scalar),
+                (0, nc.vector.tensor_copy, nc.sync),
+            ):
+                o_acc = attend_tiles(n, range(first, first + EARLY))
+                half = stage.tile([P, EARLY, D], F32, name="last_half")
+                copy(out=half[:], in_=o_acc[:])
+                queue.dma_start(
+                    out=out_rows[b][:, first : first + EARLY, h * D : (h + 1) * D], in_=half[:]
+                )
 
-        first_rows = [(x_sb[:, n, :], x_codes[:, n], x_scales[:, n]) for n in range(TILES)]
-        first_grouped = [flip_rows(rows[0], nc.vector.tensor_copy) for rows in first_rows]
-        for grouped, rows in zip(first_grouped, first_rows):
-            quantise_rows(grouped, rows[1], rows[2])
-
-        bias_all = const.tile([P, DIM], BF16)
-        for half in range(DIM // BANK):
-            cols = slice(half * BANK, (half + 1) * BANK)
-            spread = psum.tile([P, BANK], F32, tag="late%d" % half)
-            nc.tensor.matmul(out=spread[:], lhsT=ones[:], rhs=bias_row[:, cols], start=True, stop=True)
-            nc.vector.tensor_copy(out=bias_all[:, cols], in_=spread[:])
-
-        grouped_rows = {}
-        flipped_heads = {}
         quantised_p = {}
-        for n in range(len(heads) + 2):
-            grouped_rows[n] = [flip_rows(rows[0], nc.scalar.copy) for rows in row_tiles(n)]
-            if n >= 1:
-                for grouped, rows in zip(grouped_rows[n - 1], row_tiles(n - 1)):
-                    quantise_rows(grouped, rows[1], rows[2])
-            banks, flips = open_flips(*heads[n]) if n < len(heads) else (None, [])
-            if n == 0:
-                transpose_all(flips)
-                flipped_heads[n] = (copy_queries(banks["q"], nc.vector.tensor_copy), copy_keys(banks["k"]))
-            if 1 <= n <= len(heads):
-                b, h = heads[n - 1]
-                p_grouped = p_grouped_ring[(n - 1) % P_BUFFERS]
-                flipped_heads[n] = score_head(h, *flipped_heads[n - 1], p_grouped, banks, flips, nc.vector.tensor_copy if n < H else nc.scalar.copy)
+
+        amplitude_all = psum.tile([P, H], F32, tag="early")
+        bias_spread = psum.tile([P, DIM], BF16, name="bias_spread", tag="mx", bufs=2)
+        spread = [
+            (amplitude_all[:], small_row[:, DIM:]),
+            (bias_spread[:, :BANK], small_row[:, :BANK]),
+            (bias_spread[:, BANK:], small_row[:, BANK:DIM]),
+        ]
+        steps = head_steps(0, nc.vector.tensor_copy, nc.vector.tensor_copy, True)
+        for piece, (target, values) in enumerate(spread):
+            run(steps[piece * TILES : (piece + 1) * TILES])
+            nc.tensor.matmul(out=target, lhsT=ones[:], rhs=values, start=True, stop=True)
+        run(steps[len(spread) * TILES :])
+        bias_all = const.tile([P, DIM], BF16)
+
+        nc.scalar.activation(out=log_amp[:], in_=amplitude_all[:], func=ACT.Sigmoid)
+        nc.scalar.activation(out=log_amp[:], in_=log_amp[:], func=ACT.Ln)
+        nc.gpsimd.tensor_scalar_min(out=log_amp[:], in0=log_amp[:], scalar1=-1.0e-30)
+        build_decay(0)
+
+        for n in range(1, len(heads) + 1):
+            quantise_pending()
+            steps = []
+            if n < len(heads):
+                q_copy = nc.vector.tensor_copy if n < H else nc.scalar.copy
+                steps += head_steps(n, nc.vector.tensor_copy if n == 1 else nc.scalar.copy, q_copy, False)
+            if n == 1:
+                for t in range(TILES):
+                    x_copy = nc.vector.tensor_copy if t in (0, TILES - 1) else nc.scalar.copy
+                    steps += row_steps(x_sb[:, t, :], x_codes[:, t], x_scales[:, t], x_copy)
+            if n <= H:
+                t = n - 1
+                steps += row_steps(w_sb[:, t, :], w_codes[:, t], w_scales[:, t], nc.scalar.copy)
+            if TILES <= n < ROW_TILES:
+                steps += row_steps(x_sb[:, n, :], x_codes[:, n], x_scales[:, n], nc.scalar.copy)
+
+            catching_up = n >= len(heads) - 1
+            between = [2 * n - len(heads) - 1] if catching_up else []
+            score_head(n - 1, steps, between)
+            if n == 1:
+                nc.vector.tensor_copy(out=bias_all[:], in_=bias_spread[:])
             if n < H:
                 build_decay(n)
-            if 1 <= n <= len(heads):
-                v_grouped = project_values(b, h)
-                quantised_p[n - 1] = quantise_p(p_grouped)
-                quantise_v(b, h, v_grouped)
-            if n >= 2:
-                attend_head(*heads[n - 2], *quantised_p[n - 2])
+            behind = []
+            if 2 <= n < len(heads):
+                m = n - 1 if catching_up else n - 2
+                behind.append((m, project_values(m)))
+            attends = range(max(n - 3, 0), n - 2 if n < len(heads) else n - 1)
+            for m in attends[:1]:
+                attend_head(m)
+            quantise_p(n - 1)
+            for m, v_grouped in behind:
+                quantise_v(m, v_grouped)
+            for m in attends[1:]:
+                attend_head(m)
+        attend_last_head(len(heads) - 1)

from contextlib import ExitStack

import concourse.mybir as mybir
from concourse.masks import make_identity

BF16 = mybir.dt.bfloat16
F32 = mybir.dt.float32
I32 = mybir.dt.int32
U32 = mybir.dt.uint32
U8 = mybir.dt.uint8
FP8X4 = mybir.dt.float8_e4m3fn_x4
ACT = mybir.ActivationFunctionType
ALU = mybir.AluOpType

P = 128
PACK = 4
B, L, H, D = 2, 512, 8, 128
DIM = H * D
TILES = L // P
ROW_TILES = B * TILES
PASSES = DIM // (P * PACK)
BANK = 512
PARTS = 2
PAIR = 2
EARLY = 2
EARLY_SCORE_TILES = EARLY * (EARLY + 1) // 2
SCORE_TILES = [(i, j) for i in range(TILES) for j in range(i + 1)]
KEYS_FLIPPED = TILES - 1
QUERIES_FLIPPED = 2 * TILES - 1
NEVER = 1.0e38
RESULT_BUFFERS = 6
P_BUFFERS = 3

FLOPS = 2 * B * L * DIM * DIM + 2 * B * H * L * L * (2 * D) + 2 * B * H * L * L * D


def tile_retention_pb_kernel(
    tc, q_rot_re, q_rot_im, k_rot_re, k_rot_im, x, wv_w, wv_b, amplitude, out
):
    nc = tc.nc
    heads = [(b, h) for b in range(B) for h in range(H)]
    with ExitStack() as ctx:
        ctx.enter_context(tc.manual_schedule())
        const = ctx.enter_context(tc.tile_pool(name="const", bufs=1))
        inputs = ctx.enter_context(tc.tile_pool(name="inputs", bufs=1))
        keep = ctx.enter_context(tc.tile_pool(name="keep", bufs=1))
        stage = ctx.enter_context(tc.tile_pool(name="stage", bufs=2))
        psum = ctx.enter_context(tc.psum_pool(name="psum", bufs=1))

        small_row = const.tile([P, DIM + H], BF16)
        nc.vector.memset(small_row[:].bitcast(I32), 0)
        ones = const.tile([P, P], BF16)
        nc.vector.memset(ones[:], 1.0)

        p_grouped_ring = []
        for slot in range(P_BUFFERS):
            p_grouped = keep.tile([P, L, PACK], BF16, name="p_grouped%d" % slot, align_bytes=64)
            nc.vector.memset(p_grouped[:].bitcast(I32), 0)
            p_grouped_ring.append(p_grouped)

        def resident_rows(name, rows):
            return (
                inputs.tile([P, ROW_TILES, DIM], BF16, name=name),
                rows.rearrange("(n p) c -> p n c", p=P),
            )

        x_sb, x_rows = resident_rows("x_sb", x.rearrange("b l k -> (b l) k"))
        w_sb, w_rows = resident_rows("w_sb", wv_w)
        rotated = {}
        for name, tensor in (
            ("k_re", k_rot_re),
            ("k_im", k_rot_im),
            ("q_re", q_rot_re),
            ("q_im", q_rot_im),
        ):
            rotated[name] = resident_rows(name, tensor.rearrange("b l h d -> (b l) (h d)"))

        def load_heads(b, first, count, names=("k_re", "k_im", "q_re", "q_im")):
            slots = slice(b * TILES, (b + 1) * TILES)
            cols = slice(first * D, (first + count) * D)
            for name in names:
                resident, rows = rotated[name]
                nc.sync.dma_start(out=resident[:, slots, cols], in_=rows[:, slots, cols])

        def load_rows(resident, rows, tiles):
            for n in tiles:
                nc.sync.dma_start(out=resident[:, n, :], in_=rows[:, n, :])

        load_heads(0, 0, PAIR, ("k_re", "k_im"))
        nc.sync.dma_start(out=small_row[0:1, DIM:], in_=amplitude.rearrange("(o c) -> o c", o=1))
        nc.sync.dma_start(out=small_row[0:1, :DIM], in_=wv_b.rearrange("(o c) -> o c", o=1))
        load_heads(0, 0, PAIR, ("q_re", "q_im"))
        load_rows(x_sb, x_rows, range(TILES))
        for pair in range(1, H // PAIR):
            load_rows(w_sb, w_rows, range(2 * pair - 2, 2 * pair))
            load_heads(0, pair * PAIR, PAIR)
            load_rows(x_sb, x_rows, range(TILES + pair - 1, TILES + pair))
        load_rows(w_sb, w_rows, range(6, 8))
        load_rows(x_sb, x_rows, range(7, 8))
        for pair in range(H // PAIR):
            load_heads(1, pair * PAIR, PAIR)

        ident_bf16 = const.tile([P, P], BF16)
        make_identity(nc, ident_bf16[:])
        minus_ident = const.tile([P, P], BF16)
        nc.vector.tensor_scalar_mul(out=minus_ident[:], in0=ident_bf16[:], scalar1=-1.0)
        ident_f32 = const.tile([P, P], F32)
        make_identity(nc, ident_f32[:])

        farthest = (TILES - 1) * P
        distance_pattern = [[1, P], [-P, TILES]]
        distance_int = const.tile([P, P * TILES], I32)
        nc.gpsimd.iota(
            distance_int[:], pattern=distance_pattern, base=farthest, channel_multiplier=-1
        )
        distance = const.tile([P, P * TILES], F32)
        nc.vector.tensor_copy(out=distance[:], in_=distance_int[:])
        nc.gpsimd.affine_select(
            out=distance[:],
            in_=distance[:],
            pattern=distance_pattern,
            compare_op=ALU.is_ge,
            fill=NEVER,
            base=farthest,
            channel_multiplier=-1,
        )

        log_amp = const.tile([P, H], F32)
        decay = const.tile([P, H, P, TILES], F32)

        def build_decay(h):
            nc.scalar.activation(
                out=decay[:, h].rearrange("p c u -> p (c u)"),
                in_=distance[:],
                func=ACT.Exp,
                scale=log_amp[:, h : h + 1],
            )

        x_codes = keep.tile([P, ROW_TILES, PASSES, P], U32, align_bytes=64)
        x_scales = keep.tile([P, ROW_TILES, PASSES, P], U8, align_bytes=64)
        w_codes = keep.tile([P, ROW_TILES, PASSES, P], U32, align_bytes=64)
        w_scales = keep.tile([P, ROW_TILES, PASSES, P], U8, align_bytes=64)
        v_codes = keep.tile([P, B, H, D], U32, align_bytes=64)
        v_scales = keep.tile([P, B, H, D], U8, align_bytes=64)

        flipped = {}
        pending_rows = []

        def row_steps(rows_sb, codes, scales, copy):
            words = rows_sb.bitcast(F32)
            box = {}

            def step(g, u):
                if (g, u) == (0, 0):
                    box["bank"] = psum.tile([P, PASSES, 2, P], F32, name="flip_rows", tag="flip", bufs=3)
                first = (2 * g + u) * P
                nc.tensor.transpose(
                    box["bank"][:, g, u, :], words[:, first : first + P], ident_f32[:]
                )
                if (g, u) == (PASSES - 1, 1):
                    grouped = stage.tile([P, PASSES, P, PACK], BF16, align_bytes=64, bufs=5)
                    copy(
                        out=grouped[:].bitcast(F32),
                        in_=box["bank"][:].rearrange("p g u r -> p g r u"),
                    )
                    pending_rows.append((grouped, codes, scales))

            return [lambda g=g, u=u: step(g, u) for g in range(PASSES) for u in range(2)]

        def quantise_rows(grouped, codes, scales):
            nc.vector.quantize_mx(
                out=codes.rearrange("p g r -> p (g r)").bitcast(FP8X4),
                scales=scales.rearrange("p g r -> p (g r)"),
                in_=grouped[:].rearrange("p g r t -> p (g r t)"),
            )

        def quantise_pending():
            for grouped, codes, scales in pending_rows:
                quantise_rows(grouped, codes, scales)
            pending_rows.clear()

        def head_steps(n, k_copy, q_copy, by_part):
            b, h = heads[n]
            flipped[n] = {}

            def step(side, part, t, copy):
                if t == 0 and (by_part or part == 0):
                    flipped[n][side + "_bank"] = psum.tile(
                        [P, PARTS, L], BF16, name="flipped_" + side, tag="flip", bufs=3
                    )
                bank = flipped[n][side + "_bank"]
                name = side + ("_re", "_im")[part]
                target = bank[:, part, t * P : (t + 1) * P]
                natural = rotated[name][0][:, b * TILES + t, h * D : (h + 1) * D]
                if name == "k_im":
                    nc.tensor.matmul(
                        out=target, lhsT=natural, rhs=minus_ident[:], start=True, stop=True
                    )
                else:
                    nc.tensor.transpose(target, natural, ident_bf16[:])
                if t == TILES - 1 and (by_part or part == PARTS - 1):
                    if by_part:
                        if part == 0:
                            flipped[n][side] = stage.tile([P, PARTS, L], BF16, name=side + "T", bufs=3)
                        copy(out=flipped[n][side][:, part, :], in_=bank[:, part, :])
                    else:
                        flipped[n][side] = stage.tile([P, PARTS, L], BF16, name=side + "T", bufs=3)
                        copy(out=flipped[n][side][:], in_=bank[:])

            return [
                lambda side=side, part=part, t=t, copy=copy: step(side, part, t, copy)
                for side, copy in (("k", k_copy), ("q", q_copy))
                for part in range(PARTS)
                for t in range(TILES)
            ]

        def run(steps):
            for step in steps:
                step()

        def decayed(engine, h, i, s_tiles, p_grouped):
            engine.tensor_tensor(
                out=p_grouped[:, i * P : (i + 1) * P, 0 : i + 1],
                in0=s_tiles.rearrange("p j c -> p c j"),
                in1=decay[:, h, :, TILES - 1 - i : TILES],
                op=ALU.mult,
            )

        def score_head(n, steps, between):
            h = heads[n][1]
            qT, kT = flipped[n]["q"], flipped[n]["k"]
            p_grouped = p_grouped_ring[n % P_BUFFERS]
            steps = list(steps)
            early = psum.tile([P, EARLY_SCORE_TILES, P], F32, tag="early")
            late = None
            for index, (i, j) in enumerate(SCORE_TILES):
                if i >= EARLY and j == 0:
                    late = psum.tile([P, TILES, P], F32, tag="late%d" % (i - EARLY))
                for part in range(PARTS):
                    nc.tensor.matmul(
                        out=early[:, index, :] if i < EARLY else late[:, j, :],
                        lhsT=kT[:, part, j * P : (j + 1) * P],
                        rhs=qT[:, part, i * P : (i + 1) * P],
                        start=(part == 0),
                        stop=(part == PARTS - 1),
                    )
                    run(steps[:1])
                    steps = steps[1:]
                if (i, j) == (EARLY - 1, EARLY - 1):
                    early_sb = stage.tile([P, EARLY_SCORE_TILES, P], F32)
                    nc.scalar.copy(out=early_sb[:], in_=early[:])
                    for m in between:
                        quantise_v(m, project_values(m))
                    for e in range(EARLY):
                        first = e * (e + 1) // 2
                        decayed(nc.gpsimd, h, e, early_sb[:, first : first + e + 1, :], p_grouped)
                if i >= EARLY and j == i:
                    decayed(nc.vector, h, i, late[:, 0 : i + 1, :], p_grouped)
            run(steps)

        def project_values(n):
            b, h = heads[n]
            v_acc = psum.tile([P, TILES, D], F32, tag="mx", bufs=2)
            for j in range(TILES):
                for g in range(PASSES):
                    nc.tensor.matmul_mx(
                        out=v_acc[:, j, :],
                        lhsT=x_codes[:, b * TILES + j, g, :].bitcast(FP8X4),
                        lhsT_scale=x_scales[:, b * TILES + j, g, :],
                        rhs=w_codes[:, h, g, :].bitcast(FP8X4),
                        rhs_scale=w_scales[:, h, g, :],
                        start=(g == 0),
                        stop=(g == PASSES - 1),
                    )
            v_grouped = stage.tile([P, D, PACK], BF16, align_bytes=64)
            nc.vector.tensor_tensor(
                out=v_grouped[:],
                in0=v_acc[:].rearrange("p j d -> p d j"),
                in1=bias_all[:, h * D : (h + 1) * D].unsqueeze(2).to_broadcast([P, D, PACK]),
                op=ALU.add,
            )
            return v_grouped

        def quantise_p(n):
            p_grouped = p_grouped_ring[n % P_BUFFERS]
            p_codes = stage.tile([P, L], U32, align_bytes=64, bufs=4)
            p_scales = stage.tile([P, L], U8, align_bytes=64, bufs=4)
            for first in (EARLY * P, 0):
                cols = slice(first, first + EARLY * P)
                nc.vector.quantize_mx(
                    out=p_codes[:, cols].bitcast(FP8X4),
                    scales=p_scales[:, cols],
                    in_=p_grouped[:, cols, :].rearrange("p l j -> p (l j)"),
                )
            quantised_p[n] = (p_codes, p_scales)

        def quantise_v(n, v_grouped):
            b, h = heads[n]
            nc.vector.quantize_mx(
                out=v_codes[:, b, h, :].bitcast(FP8X4),
                scales=v_scales[:, b, h, :],
                in_=v_grouped[:].rearrange("p d j -> p (d j)"),
            )

        out_rows = out.rearrange("b (i p) c -> b p i c", p=P)
        results = {}

        def attend_tiles(n, tiles):
            b, h = heads[n]
            p_codes, p_scales = quantised_p[n]
            o_acc = psum.tile([P, len(tiles), D], F32, name="o_acc", tag="mx", bufs=2)
            for place, i in enumerate(tiles):
                nc.tensor.matmul_mx(
                    out=o_acc[:, place, :],
                    lhsT=p_codes[:, i * P : (i + 1) * P].bitcast(FP8X4),
                    lhsT_scale=p_scales[:, i * P : (i + 1) * P],
                    rhs=v_codes[:, b, h, :].bitcast(FP8X4),
                    rhs_scale=v_scales[:, b, h, :],
                    start=True,
                    stop=True,
                )
            return o_acc

        def attend_head(n):
            b, h = heads[n]
            o_acc = attend_tiles(n, range(TILES))
            member = h % PAIR
            if member == 0:
                results["tile"] = stage.tile([P, TILES, PAIR, D], F32, name="result", bufs=RESULT_BUFFERS)
            result = results["tile"]
            nc.scalar.copy(out=result[:, :, member, :], in_=o_acc[:])
            if n == len(heads) - 2:
                nc.sync.dma_start(
                    out=out_rows[b][:, :, h * D : (h + 1) * D], in_=result[:, :, member, :]
                )
            elif member == PAIR - 1:
                first = (h - member) * D
                nc.sync.dma_start(
                    out=out_rows[b][:, :, first : first + PAIR * D],
                    in_=result[:].rearrange("p i g d -> p i (g d)"),
                )

        def attend_last_head(n):
            b, h = heads[n]
            for first, copy, queue in (
                (EARLY, nc.scalar.copy, nc.scalar),
                (0, nc.vector.tensor_copy, nc.sync),
            ):
                o_acc = attend_tiles(n, range(first, first + EARLY))
                half = stage.tile([P, EARLY, D], F32, name="last_half")
                copy(out=half[:], in_=o_acc[:])
                queue.dma_start(
                    out=out_rows[b][:, first : first + EARLY, h * D : (h + 1) * D], in_=half[:]
                )

        quantised_p = {}

        amplitude_all = psum.tile([P, H], F32, tag="early")
        bias_spread = psum.tile([P, DIM], BF16, name="bias_spread", tag="mx", bufs=2)
        spread = [
            (amplitude_all[:], small_row[:, DIM:]),
            (bias_spread[:, :BANK], small_row[:, :BANK]),
            (bias_spread[:, BANK:], small_row[:, BANK:DIM]),
        ]
        steps = head_steps(0, nc.vector.tensor_copy, nc.vector.tensor_copy, True)
        for piece, (target, values) in enumerate(spread):
            run(steps[piece * TILES : (piece + 1) * TILES])
            nc.tensor.matmul(out=target, lhsT=ones[:], rhs=values, start=True, stop=True)
        run(steps[len(spread) * TILES :])
        bias_all = const.tile([P, DIM], BF16)

        nc.scalar.activation(out=log_amp[:], in_=amplitude_all[:], func=ACT.Sigmoid)
        nc.scalar.activation(out=log_amp[:], in_=log_amp[:], func=ACT.Ln)
        nc.gpsimd.tensor_scalar_min(out=log_amp[:], in0=log_amp[:], scalar1=-1.0e-30)
        build_decay(0)

        for n in range(1, len(heads) + 1):
            quantise_pending()
            steps = []
            if n < len(heads):
                q_copy = nc.vector.tensor_copy if n < H else nc.scalar.copy
                steps += head_steps(n, nc.vector.tensor_copy if n == 1 else nc.scalar.copy, q_copy, False)
            if n == 1:
                for t in range(TILES):
                    x_copy = nc.vector.tensor_copy if t in (0, TILES - 1) else nc.scalar.copy
                    steps += row_steps(x_sb[:, t, :], x_codes[:, t], x_scales[:, t], x_copy)
            if n <= H:
                t = n - 1
                steps += row_steps(w_sb[:, t, :], w_codes[:, t], w_scales[:, t], nc.scalar.copy)
            if TILES <= n < ROW_TILES:
                steps += row_steps(x_sb[:, n, :], x_codes[:, n], x_scales[:, n], nc.scalar.copy)

            catching_up = n >= len(heads) - 1
            between = [2 * n - len(heads) - 1] if catching_up else []
            score_head(n - 1, steps, between)
            if n == 1:
                nc.vector.tensor_copy(out=bias_all[:], in_=bias_spread[:])
            if n < H:
                build_decay(n)
            behind = []
            if 2 <= n < len(heads):
                m = n - 1 if catching_up else n - 2
                behind.append((m, project_values(m)))
            attends = range(max(n - 3, 0), n - 2 if n < len(heads) else n - 1)
            for m in attends[:1]:
                attend_head(m)
            quantise_p(n - 1)
            for m, v_grouped in behind:
                quantise_v(m, v_grouped)
            for m in attends[1:]:
                attend_head(m)
        attend_last_head(len(heads) - 1)
